import numpy as np
import ml_dtypes


def mxq(x, axis, fmt="e4m3"):
    dtype, down = {"e4m3": (ml_dtypes.float8_e4m3fn, 7), "e5m2": (ml_dtypes.float8_e5m2, 14)}[fmt]
    v = np.moveaxis(np.asarray(x, np.float32).astype(ml_dtypes.bfloat16).astype(np.float64), axis, -1)
    blocks = v.reshape(v.shape[:-1] + (-1, 32))
    amax = np.abs(blocks).max(-1, keepdims=True)
    byte = np.maximum(np.where(amax > 0, np.frexp(amax)[1] - 1 + 127, 0) - down, 1)
    scale = np.exp2(byte - 127.0)
    codes = (blocks / scale).astype(np.float32).astype(dtype).astype(np.float64)
    return np.moveaxis((codes * scale).reshape(v.shape), -1, axis)


WIDE = False


def mx_kscale(k):
    if not WIDE:
        return np.ones(k)
    levels = np.array([10, -10, 5, -5, 0])
    a = np.random.permutation(np.resize(levels, k // 512 * 4)).reshape(k // 512, 4)
    idx = np.arange(k)
    return np.exp2(a[idx // 512, idx % 128 // 32])


BF16 = ml_dtypes.bfloat16


def bf(x):
    return np.asarray(x, np.float32).astype(BF16)


def f64(x):
    return np.asarray(x).astype(np.float64)


B, H, C = 1024, 2048, 1024
GAMMA = 100.0
EPS = 1e-8


def softmax(v):
    e = np.exp(v - v.max(axis=1, keepdims=True))
    return e / e.sum(axis=1, keepdims=True)


def setup_inputs():
    t = mx_kscale(C)
    t = t / t.min()
    u = np.random.random((C, H))
    near = np.flatnonzero(t == 1.0)
    lab = near[np.random.randint(0, near.size, B)]
    lean = (np.log(C) + GAMMA**2 / (8.0 * H)) * 4.0 * np.sqrt(3.0) / GAMMA
    x = np.random.standard_normal((B, H)) + lean * (u[lab] - 0.5)
    return {"X": bf(x * 130.0 / np.sqrt(H)), "grp": bf(u * t[:, None] * 225.0 / np.sqrt(H))}


def reference(X, grp):
    X, grp = f64(X), f64(grp)
    dot = mxq(X, 1, "e4m3") @ mxq(grp, 1, "e4m3").T
    x_sq = np.sum(X * X, axis=1)
    g_sq = np.sum(grp * grp, axis=1)
    x_nrm = np.sqrt(x_sq)
    g_nrm = np.sqrt(g_sq)
    cos = dot / np.maximum(x_nrm[:, None] * g_nrm[None, :], EPS)
    cs = softmax(GAMMA * cos)
    d2 = np.maximum(x_sq[:, None] + g_sq[None, :] - 2.0 * dot, 0.0)
    d = np.sqrt(d2)
    norm_w = softmax(-d)
    return cs * norm_w

@@ -1,0 +1,269 @@
+from contextlib import ExitStack
+
+import concourse.mybir as mybir
+from concourse.masks import make_identity
+
+F32 = mybir.dt.float32
+BF16 = mybir.dt.bfloat16
+U32 = mybir.dt.uint32
+U8 = mybir.dt.uint8
+FP8X4 = mybir.dt.float8_e4m3fn_x4
+ACT = mybir.ActivationFunctionType
+ALU = mybir.AluOpType
+
+P = 128
+B, H, C = 1024, 2048, 1024
+ROW_TILES = B // P
+K_PASS = 4 * P
+PASSES = H // K_PASS
+WORDS = H // 2
+N_MOVE = 512
+HALVES = C // N_MOVE
+
+GAMMA = 100.0
+EPS = 1e-8
+TINY_SQ = 1e-30
+TINY_D2 = 1e-30
+CENTRE = 1.875
+WINDOW = 4.0
+
+FLOPS = 2 * B * C * H
+
+
+def transpose_and_regroup(nc, psum, stage, natural, ident):
+    words = natural.bitcast(F32)
+    grouped = stage.tile([P, 4 * PASSES * P], BF16, align_bytes=64, name="grouped")
+    grouped_words = grouped[:].bitcast(F32).rearrange("p (g r u) -> p g r u", g=PASSES, u=2)
+    for bank in range(2):
+        flipped = psum.tile([P, 4, P], F32, name="flipped", tag="flipped")
+        for w in range(4):
+            first = (4 * bank + w) * P
+            nc.tensor.transpose(flipped[:, w, :], words[:, first : first + P], ident[:])
+        source = flipped[:].rearrange("p (g u) r -> p g r u", u=2)
+        target = grouped_words[:, 2 * bank : 2 * bank + 2]
+        nc.vector.tensor_copy(out=target, in_=source)
+    return grouped
+
+
+def inverse_norms(nc, small, squares, name):
+    safe = small.tile([P, ROW_TILES], F32, name=name + "_safe")
+    nc.vector.tensor_scalar_max(out=safe[:], in0=squares[:], scalar1=TINY_SQ)
+    rough = small.tile([P, ROW_TILES], F32, name=name + "_rough")
+    nc.scalar.activation(out=rough[:], in_=safe[:], func=ACT.Sqrt)
+    guess = small.tile([P, ROW_TILES], F32, name=name + "_guess")
+    nc.vector.reciprocal(out=guess[:], in_=rough[:])
+    ratio = small.tile([P, ROW_TILES], F32, name=name + "_ratio")
+    nc.vector.tensor_mul(out=ratio[:], in0=guess[:], in1=guess[:])
+    nc.vector.tensor_mul(out=ratio[:], in0=ratio[:], in1=safe[:])
+    nc.vector.tensor_scalar(
+        out=ratio[:], in0=ratio[:], scalar1=-0.5, scalar2=1.5, op0=ALU.mult, op1=ALU.add
+    )
+    inverse = small.tile([P, ROW_TILES], F32, name=name + "_inverse")
+    nc.vector.tensor_mul(out=inverse[:], in0=guess[:], in1=ratio[:])
+    return inverse
+
+
+def spread_over_partitions(nc, psum, keep, per_class, ident, name):
+    repeated = keep.tile([P, ROW_TILES, P], F32, name=name + "_repeated")
+    nc.vector.tensor_copy(
+        out=repeated[:], in_=per_class[:].unsqueeze(2).to_broadcast([P, ROW_TILES, P])
+    )
+    spread = keep.tile([P, C], F32, name=name + "_spread")
+    for h in range(HALVES):
+        flipped = psum.tile([P, 4, P], F32, name="flipped", tag="flipped")
+        for w in range(4):
+            nc.tensor.transpose(flipped[:, w, :], repeated[:, 4 * h + w, :], ident[:])
+        nc.vector.tensor_copy(
+            out=spread[:, N_MOVE * h : N_MOVE * (h + 1)],
+            in_=flipped[:].rearrange("p w c -> p (w c)"),
+        )
+    return spread
+
+
+def tile_classifier_kernel(tc, X, grp, out):
+    nc = tc.nc
+    with ExitStack() as ctx:
+        keep = ctx.enter_context(tc.tile_pool(name="keep", bufs=1))
+        small = ctx.enter_context(tc.tile_pool(name="small", bufs=1))
+        stage = ctx.enter_context(tc.tile_pool(name="stage", bufs=3))
+        scrap = ctx.enter_context(tc.tile_pool(name="scrap", bufs=2))
+        psum_t = ctx.enter_context(tc.psum_pool(name="psum_t", bufs=4))
+        psum_d = ctx.enter_context(tc.psum_pool(name="psum_d", bufs=4))
+
+        g_nat = keep.tile([P, ROW_TILES, H], BF16, name="g_nat")
+        x_nat = keep.tile([P, ROW_TILES, H], BF16, name="x_nat")
+        for j in range(ROW_TILES):
+            nc.sync.dma_start(out=g_nat[:, j, :], in_=grp[P * j : P * (j + 1), :])
+        for i in range(ROW_TILES):
+            nc.sync.dma_start(out=x_nat[:, i, :], in_=X[P * i : P * (i + 1), :])
+
+        ident = keep.tile([P, P], F32, name="ident")
+        make_identity(nc, ident[:])
+
+        warm = small.tile([P, 1], F32, name="warm")
+        nc.vector.memset(warm[:], 1.0)
+        nc.scalar.activation(out=warm[:], in_=warm[:], func=ACT.Sqrt)
+
+        g_codes = keep.tile([P, PASSES, C], U32, align_bytes=64, name="g_codes")
+        g_scales = keep.tile([P, PASSES, C], U8, align_bytes=64, name="g_scales")
+        x_codes = keep.tile([P, ROW_TILES, PASSES * P], U32, align_bytes=64, name="x_codes")
+        x_scales = keep.tile([P, ROW_TILES, PASSES * P], U8, align_bytes=64, name="x_scales")
+
+        g_sq = small.tile([P, ROW_TILES], F32, name="g_sq")
+        for j in range(ROW_TILES):
+            squares = scrap.tile([P, H], BF16, name="squares")
+            nc.scalar.activation(
+                out=squares[:], in_=g_nat[:, j, :], func=ACT.Square, accum_out=g_sq[:, j : j + 1]
+            )
+            grouped = transpose_and_regroup(nc, psum_t, stage, g_nat[:, j, :], ident)
+            for g in range(PASSES):
+                cols = slice(P * j, P * (j + 1))
+                nc.vector.quantize_mx(
+                    out=g_codes[:, g, cols].bitcast(FP8X4),
+                    scales=g_scales[:, g, cols],
+                    in_=grouped[:, K_PASS * g : K_PASS * (g + 1)],
+                )
+        g_half = small.tile([P, ROW_TILES], F32, name="g_half")
+        nc.vector.tensor_scalar_mul(out=g_half[:], in0=g_sq[:], scalar1=0.5)
+        g_inv = inverse_norms(nc, small, g_sq, "g")
+        g_half_all = spread_over_partitions(nc, psum_t, keep, g_half, ident, "g_half")
+        g_inv_all = spread_over_partitions(nc, psum_t, keep, g_inv, ident, "g_inv")
+
+        cosine = keep.tile([P, ROW_TILES, C], F32, name="cosine")
+        dist = keep.tile([P, ROW_TILES, C], F32, name="dist")
+        x_sq = small.tile([P, ROW_TILES], F32, name="x_sq")
+        x_half = small.tile([P, ROW_TILES], F32, name="x_half")
+        x_cap = small.tile([P, ROW_TILES], F32, name="x_cap")
+        x_safe = small.tile([P, ROW_TILES], F32, name="x_safe")
+        least = small.tile([P, ROW_TILES], F32, name="least")
+        nearest = small.tile([P, ROW_TILES], F32, name="nearest")
+        step = small.tile([P, ROW_TILES], F32, name="step")
+        unit = small.tile([P, ROW_TILES], F32, name="unit")
+        zoom = small.tile([P, ROW_TILES], F32, name="zoom")
+        for i in range(ROW_TILES):
+            col = slice(i, i + 1)
+            squares = scrap.tile([P, H], BF16, name="squares")
+            nc.scalar.activation(
+                out=squares[:], in_=x_nat[:, i, :], func=ACT.Square, accum_out=x_sq[:, col]
+            )
+            nc.vector.tensor_scalar_mul(out=x_half[:, col], in0=x_sq[:, col], scalar1=0.5)
+            nc.vector.tensor_scalar_max(out=x_safe[:, col], in0=x_sq[:, col], scalar1=TINY_SQ)
+            nc.scalar.activation(
+                out=x_cap[:, col], in_=x_safe[:, col], func=ACT.Sqrt, scale=1.0 / (EPS * EPS)
+            )
+            grouped = transpose_and_regroup(nc, psum_t, stage, x_nat[:, i, :], ident)
+            nc.vector.quantize_mx(
+                out=x_codes[:, i, :].bitcast(FP8X4), scales=x_scales[:, i, :], in_=grouped[:]
+            )
+            for h in range(HALVES):
+                cols = slice(N_MOVE * h, N_MOVE * (h + 1))
+                dot = psum_d.tile([P, N_MOVE], F32, name="dot")
+                for g in range(PASSES):
+                    rows = slice(P * g, P * (g + 1))
+                    nc.tensor.matmul_mx(
+                        out=dot[:],
+                        lhsT=x_codes[:, i, rows].bitcast(FP8X4),
+                        lhsT_scale=x_scales[:, i, rows],
+                        rhs=g_codes[:, g, cols].bitcast(FP8X4),
+                        rhs_scale=g_scales[:, g, cols],
+                        start=(g == 0),
+                        stop=(g == PASSES - 1),
+                    )
+                nc.vector.scalar_tensor_tensor(
+                    out=cosine[:, i, cols],
+                    in0=g_inv_all[:, cols],
+                    scalar=x_cap[:, col],
+                    in1=dot[:],
+                    op0=ALU.min,
+                    op1=ALU.mult,
+                )
+                nc.vector.scalar_tensor_tensor(
+                    out=dist[:, i, cols],
+                    in0=g_half_all[:, cols],
+                    scalar=x_half[:, col],
+                    in1=dot[:],
+                    op0=ALU.add,
+                    op1=ALU.subtract,
+                )
+            nc.vector.tensor_scalar(
+                out=dist[:, i, :],
+                in0=dist[:, i, :],
+                scalar1=TINY_D2,
+                scalar2=None,
+                op0=ALU.max,
+                op1=ALU.min,
+                accum_out=least[:, col],
+            )
+            nc.scalar.activation(
+                out=nearest[:, col], in_=least[:, col], func=ACT.Sqrt, scale=2.0
+            )
+            nc.vector.tensor_scalar(
+                out=step[:, col],
+                in0=nearest[:, col],
+                scalar1=WINDOW,
+                scalar2=CENTRE**-0.5,
+                op0=ALU.add,
+                op1=ALU.mult,
+            )
+            nc.vector.tensor_scalar(
+                out=unit[:, col],
+                in0=step[:, col],
+                scalar1=0.5,
+                scalar2=step[:, col],
+                op0=ALU.mult,
+                op1=ALU.mult,
+            )
+            nc.vector.reciprocal(out=zoom[:, col], in_=unit[:, col])
+            nc.scalar.activation(
+                out=dist[:, i, :], in_=dist[:, i, :], func=ACT.Sqrt, scale=zoom[:, col]
+            )
+
+        x_inv = inverse_norms(nc, small, x_sq, "x")
+        minus_gamma = small.tile([P, ROW_TILES], F32, name="minus_gamma")
+        nc.vector.tensor_scalar_mul(out=minus_gamma[:], in0=x_inv[:], scalar1=-GAMMA)
+        minus_step = small.tile([P, ROW_TILES], F32, name="minus_step")
+        nc.vector.tensor_scalar_mul(out=minus_step[:], in0=step[:], scalar1=-1.0)
+
+        minus_top = small.tile([P, ROW_TILES], F32, name="minus_top")
+        sum_cos = small.tile([P, ROW_TILES], F32, name="sum_cos")
+        sum_dist = small.tile([P, ROW_TILES], F32, name="sum_dist")
+        sums = small.tile([P, ROW_TILES], F32, name="sums")
+        norm = small.tile([P, ROW_TILES], F32, name="norm")
+        for i in range(ROW_TILES):
+            col = slice(i, i + 1)
+            nc.vector.tensor_scalar(
+                out=cosine[:, i, :],
+                in0=cosine[:, i, :],
+                scalar1=minus_gamma[:, col],
+                scalar2=None,
+                op0=ALU.mult,
+                op1=ALU.min,
+                accum_out=minus_top[:, col],
+            )
+            nc.scalar.activation(
+                out=cosine[:, i, :],
+                in_=cosine[:, i, :],
+                func=ACT.Exp,
+                scale=-1.0,
+                bias=minus_top[:, col],
+                accum_out=sum_cos[:, col],
+            )
+            nc.scalar.activation(
+                out=dist[:, i, :],
+                in_=dist[:, i, :],
+                func=ACT.Exp,
+                scale=minus_step[:, col],
+                bias=nearest[:, col],
+                accum_out=sum_dist[:, col],
+            )
+            nc.vector.tensor_mul(out=sums[:, col], in0=sum_cos[:, col], in1=sum_dist[:, col])
+            nc.vector.reciprocal(out=norm[:, col], in_=sums[:, col])
+            nc.vector.scalar_tensor_tensor(
+                out=cosine[:, i, :],
+                in0=cosine[:, i, :],
+                scalar=norm[:, col],
+                in1=dist[:, i, :],
+                op0=ALU.mult,
+                op1=ALU.mult,
+            )
+            nc.sync.dma_start(out=out[P * i : P * (i + 1), :], in_=cosine[:, i, :])

@@ -16,9 +16,9 @@ B, H, C = 1024, 2048, 1024
 ROW_TILES = B // P
 K_PASS = 4 * P
 PASSES = H // K_PASS
-WORDS = H // 2
 N_MOVE = 512
 HALVES = C // N_MOVE
+AHEAD = 2
 
 GAMMA = 100.0
 EPS = 1e-8
@@ -30,26 +30,30 @@ WINDOW = 4.0
 FLOPS = 2 * B * C * H
 
 
-def transpose_and_regroup(nc, psum, stage, natural, ident):
+def transposes(nc, psum, natural, ident):
     words = natural.bitcast(F32)
-    grouped = stage.tile([P, 4 * PASSES * P], BF16, align_bytes=64, name="grouped")
-    grouped_words = grouped[:].bitcast(F32).rearrange("p (g r u) -> p g r u", g=PASSES, u=2)
+    banks = []
     for bank in range(2):
         flipped = psum.tile([P, 4, P], F32, name="flipped", tag="flipped")
         for w in range(4):
             first = (4 * bank + w) * P
             nc.tensor.transpose(flipped[:, w, :], words[:, first : first + P], ident[:])
-        source = flipped[:].rearrange("p (g u) r -> p g r u", u=2)
-        target = grouped_words[:, 2 * bank : 2 * bank + 2]
-        nc.vector.tensor_copy(out=target, in_=source)
+        banks.append(flipped)
+    return banks
+
+
+def regroup(copy, stage, banks):
+    grouped = stage.tile([P, 4 * PASSES * P], BF16, align_bytes=64, name="grouped")
+    grouped_words = grouped[:].bitcast(F32).rearrange("p (g r u) -> p g r u", g=PASSES, u=2)
+    for bank in range(2):
+        copy(
+            out=grouped_words[:, 2 * bank : 2 * bank + 2],
+            in_=banks[bank][:].rearrange("p (g u) r -> p g r u", u=2),
+        )
     return grouped
 
 
-def inverse_norms(nc, small, squares, name):
-    safe = small.tile([P, ROW_TILES], F32, name=name + "_safe")
-    nc.vector.tensor_scalar_max(out=safe[:], in0=squares[:], scalar1=TINY_SQ)
-    rough = small.tile([P, ROW_TILES], F32, name=name + "_rough")
-    nc.scalar.activation(out=rough[:], in_=safe[:], func=ACT.Sqrt)
+def newton_inverse_root(nc, small, safe, rough, name):
     guess = small.tile([P, ROW_TILES], F32, name=name + "_guess")
     nc.vector.reciprocal(out=guess[:], in_=rough[:])
     ratio = small.tile([P, ROW_TILES], F32, name=name + "_ratio")
@@ -64,15 +68,14 @@ def inverse_norms(nc, small, squares, name):
 
 
 def spread_over_partitions(nc, psum, keep, per_class, ident, name):
-    repeated = keep.tile([P, ROW_TILES, P], F32, name=name + "_repeated")
-    nc.vector.tensor_copy(
-        out=repeated[:], in_=per_class[:].unsqueeze(2).to_broadcast([P, ROW_TILES, P])
-    )
     spread = keep.tile([P, C], F32, name=name + "_spread")
     for h in range(HALVES):
         flipped = psum.tile([P, 4, P], F32, name="flipped", tag="flipped")
         for w in range(4):
-            nc.tensor.transpose(flipped[:, w, :], repeated[:, 4 * h + w, :], ident[:])
+            j = 4 * h + w
+            nc.tensor.transpose(
+                flipped[:, w, :], per_class[:, j : j + 1].to_broadcast([P, P]), ident[:]
+            )
         nc.vector.tensor_copy(
             out=spread[:, N_MOVE * h : N_MOVE * (h + 1)],
             in_=flipped[:].rearrange("p w c -> p (w c)"),
@@ -89,6 +92,7 @@ def tile_classifier_kernel(tc, X, grp, out):
         scrap = ctx.enter_context(tc.tile_pool(name="scrap", bufs=2))
         psum_t = ctx.enter_context(tc.psum_pool(name="psum_t", bufs=4))
         psum_d = ctx.enter_context(tc.psum_pool(name="psum_d", bufs=4))
+        ctx.enter_context(tc.manual_schedule())
 
         g_nat = keep.tile([P, ROW_TILES, H], BF16, name="g_nat")
         x_nat = keep.tile([P, ROW_TILES, H], BF16, name="x_nat")
@@ -102,59 +106,60 @@ def tile_classifier_kernel(tc, X, grp, out):
 
         warm = small.tile([P, 1], F32, name="warm")
         nc.vector.memset(warm[:], 1.0)
+        floor = small.tile([P, 1], F32, name="floor")
+        nc.vector.memset(floor[:], TINY_SQ / (EPS * EPS))
         nc.scalar.activation(out=warm[:], in_=warm[:], func=ACT.Sqrt)
 
         g_codes = keep.tile([P, PASSES, C], U32, align_bytes=64, name="g_codes")
         g_scales = keep.tile([P, PASSES, C], U8, align_bytes=64, name="g_scales")
         x_codes = keep.tile([P, ROW_TILES, PASSES * P], U32, align_bytes=64, name="x_codes")
         x_scales = keep.tile([P, ROW_TILES, PASSES * P], U8, align_bytes=64, name="x_scales")
+        cosine = keep.tile([P, ROW_TILES, C], F32, name="cosine")
+        dist = keep.tile([P, ROW_TILES, C], F32, name="dist")
 
-        g_sq = small.tile([P, ROW_TILES], F32, name="g_sq")
-        for j in range(ROW_TILES):
+        def stat(name):
+            return small.tile([P, ROW_TILES], F32, name=name)
+
+        g_sq, g_half, g_safe, g_rough = stat("g_sq"), stat("g_half"), stat("g_safe"), stat("g_rough")
+        x_sq, x_half, x_cap = stat("x_sq"), stat("x_half"), stat("x_cap")
+        x_safe, x_rough = stat("x_safe"), stat("x_rough")
+        least, nearest, step, unit, zoom = (
+            stat("least"), stat("nearest"), stat("step"), stat("unit"), stat("zoom"),
+        )
+        minus_gamma, minus_step, minus_top = (
+            stat("minus_gamma"), stat("minus_step"), stat("minus_top"),
+        )
+        sum_cos, sum_dist, sums, norm = stat("sum_cos"), stat("sum_dist"), stat("sums"), stat("norm")
+
+        def sum_of_squares(natural, total):
             squares = scrap.tile([P, H], BF16, name="squares")
-            nc.scalar.activation(
-                out=squares[:], in_=g_nat[:, j, :], func=ACT.Square, accum_out=g_sq[:, j : j + 1]
-            )
-            grouped = transpose_and_regroup(nc, psum_t, stage, g_nat[:, j, :], ident)
+            nc.scalar.activation(out=squares[:], in_=natural, func=ACT.Square, accum_out=total)
+
+        def quantise_classes(j, grouped):
+            cols = slice(P * j, P * (j + 1))
             for g in range(PASSES):
-                cols = slice(P * j, P * (j + 1))
                 nc.vector.quantize_mx(
                     out=g_codes[:, g, cols].bitcast(FP8X4),
                     scales=g_scales[:, g, cols],
                     in_=grouped[:, K_PASS * g : K_PASS * (g + 1)],
                 )
-        g_half = small.tile([P, ROW_TILES], F32, name="g_half")
-        nc.vector.tensor_scalar_mul(out=g_half[:], in0=g_sq[:], scalar1=0.5)
-        g_inv = inverse_norms(nc, small, g_sq, "g")
-        g_half_all = spread_over_partitions(nc, psum_t, keep, g_half, ident, "g_half")
-        g_inv_all = spread_over_partitions(nc, psum_t, keep, g_inv, ident, "g_inv")
 
-        cosine = keep.tile([P, ROW_TILES, C], F32, name="cosine")
-        dist = keep.tile([P, ROW_TILES, C], F32, name="dist")
-        x_sq = small.tile([P, ROW_TILES], F32, name="x_sq")
-        x_half = small.tile([P, ROW_TILES], F32, name="x_half")
-        x_cap = small.tile([P, ROW_TILES], F32, name="x_cap")
-        x_safe = small.tile([P, ROW_TILES], F32, name="x_safe")
-        least = small.tile([P, ROW_TILES], F32, name="least")
-        nearest = small.tile([P, ROW_TILES], F32, name="nearest")
-        step = small.tile([P, ROW_TILES], F32, name="step")
-        unit = small.tile([P, ROW_TILES], F32, name="unit")
-        zoom = small.tile([P, ROW_TILES], F32, name="zoom")
-        for i in range(ROW_TILES):
-            col = slice(i, i + 1)
-            squares = scrap.tile([P, H], BF16, name="squares")
-            nc.scalar.activation(
-                out=squares[:], in_=x_nat[:, i, :], func=ACT.Square, accum_out=x_sq[:, col]
-            )
-            nc.vector.tensor_scalar_mul(out=x_half[:, col], in0=x_sq[:, col], scalar1=0.5)
-            nc.vector.tensor_scalar_max(out=x_safe[:, col], in0=x_sq[:, col], scalar1=TINY_SQ)
-            nc.scalar.activation(
-                out=x_cap[:, col], in_=x_safe[:, col], func=ACT.Sqrt, scale=1.0 / (EPS * EPS)
-            )
-            grouped = transpose_and_regroup(nc, psum_t, stage, x_nat[:, i, :], ident)
+        def quantise_rows(i, grouped):
             nc.vector.quantize_mx(
                 out=x_codes[:, i, :].bitcast(FP8X4), scales=x_scales[:, i, :], in_=grouped[:]
             )
+
+        def row_norms(i):
+            col = slice(i, i + 1)
+            sum_of_squares(x_nat[:, i, :], x_sq[:, col])
+            nc.scalar.mul(out=x_half[:, col], in_=x_sq[:, col], mul=0.5)
+            nc.scalar.activation(
+                out=x_cap[:, col], in_=x_sq[:, col], func=ACT.Sqrt,
+                scale=1.0 / (EPS * EPS), bias=floor[:],
+            )
+
+        def products(i):
+            dots = []
             for h in range(HALVES):
                 cols = slice(N_MOVE * h, N_MOVE * (h + 1))
                 dot = psum_d.tile([P, N_MOVE], F32, name="dot")
@@ -169,101 +174,128 @@ def tile_classifier_kernel(tc, X, grp, out):
                         start=(g == 0),
                         stop=(g == PASSES - 1),
                     )
+                dots.append(dot)
+            return dots
+
+        def cosine_and_distance(i, dots):
+            col = slice(i, i + 1)
+            for h in range(HALVES):
+                cols = slice(N_MOVE * h, N_MOVE * (h + 1))
                 nc.vector.scalar_tensor_tensor(
-                    out=cosine[:, i, cols],
-                    in0=g_inv_all[:, cols],
-                    scalar=x_cap[:, col],
-                    in1=dot[:],
-                    op0=ALU.min,
-                    op1=ALU.mult,
+                    out=cosine[:, i, cols], in0=g_inv_all[:, cols], scalar=x_cap[:, col],
+                    in1=dots[h][:], op0=ALU.min, op1=ALU.mult,
                 )
                 nc.vector.scalar_tensor_tensor(
-                    out=dist[:, i, cols],
-                    in0=g_half_all[:, cols],
-                    scalar=x_half[:, col],
-                    in1=dot[:],
-                    op0=ALU.add,
-                    op1=ALU.subtract,
+                    out=dist[:, i, cols], in0=g_half_all[:, cols], scalar=x_half[:, col],
+                    in1=dots[h][:], op0=ALU.add, op1=ALU.subtract,
                 )
+
+        def clamp_and_least(i):
             nc.vector.tensor_scalar(
-                out=dist[:, i, :],
-                in0=dist[:, i, :],
-                scalar1=TINY_D2,
-                scalar2=None,
-                op0=ALU.max,
-                op1=ALU.min,
-                accum_out=least[:, col],
-            )
-            nc.scalar.activation(
-                out=nearest[:, col], in_=least[:, col], func=ACT.Sqrt, scale=2.0
-            )
-            nc.vector.tensor_scalar(
-                out=step[:, col],
-                in0=nearest[:, col],
-                scalar1=WINDOW,
-                scalar2=CENTRE**-0.5,
-                op0=ALU.add,
-                op1=ALU.mult,
-            )
-            nc.vector.tensor_scalar(
-                out=unit[:, col],
-                in0=step[:, col],
-                scalar1=0.5,
-                scalar2=step[:, col],
-                op0=ALU.mult,
-                op1=ALU.mult,
-            )
-            nc.vector.reciprocal(out=zoom[:, col], in_=unit[:, col])
-            nc.scalar.activation(
-                out=dist[:, i, :], in_=dist[:, i, :], func=ACT.Sqrt, scale=zoom[:, col]
+                out=dist[:, i, :], in0=dist[:, i, :], scalar1=TINY_D2, scalar2=None,
+                op0=ALU.max, op1=ALU.min, accum_out=least[:, i : i + 1],
             )
 
-        x_inv = inverse_norms(nc, small, x_sq, "x")
-        minus_gamma = small.tile([P, ROW_TILES], F32, name="minus_gamma")
-        nc.vector.tensor_scalar_mul(out=minus_gamma[:], in0=x_inv[:], scalar1=-GAMMA)
-        minus_step = small.tile([P, ROW_TILES], F32, name="minus_step")
-        nc.vector.tensor_scalar_mul(out=minus_step[:], in0=step[:], scalar1=-1.0)
+        def nearest_distance(i):
+            col = slice(i, i + 1)
+            nc.scalar.activation(out=nearest[:, col], in_=least[:, col], func=ACT.Sqrt, scale=2.0)
 
-        minus_top = small.tile([P, ROW_TILES], F32, name="minus_top")
-        sum_cos = small.tile([P, ROW_TILES], F32, name="sum_cos")
-        sum_dist = small.tile([P, ROW_TILES], F32, name="sum_dist")
-        sums = small.tile([P, ROW_TILES], F32, name="sums")
-        norm = small.tile([P, ROW_TILES], F32, name="norm")
-        for i in range(ROW_TILES):
+        def window(i):
             col = slice(i, i + 1)
             nc.vector.tensor_scalar(
-                out=cosine[:, i, :],
-                in0=cosine[:, i, :],
-                scalar1=minus_gamma[:, col],
-                scalar2=None,
-                op0=ALU.mult,
-                op1=ALU.min,
-                accum_out=minus_top[:, col],
+                out=step[:, col], in0=nearest[:, col], scalar1=WINDOW, scalar2=CENTRE**-0.5,
+                op0=ALU.add, op1=ALU.mult,
+            )
+            nc.vector.tensor_scalar(
+                out=unit[:, col], in0=step[:, col], scalar1=0.5, scalar2=step[:, col],
+                op0=ALU.mult, op1=ALU.mult,
+            )
+            nc.vector.reciprocal(out=zoom[:, col], in_=unit[:, col])
+
+        def root(i):
+            nc.scalar.activation(
+                out=dist[:, i, :], in_=dist[:, i, :], func=ACT.Sqrt, scale=zoom[:, i : i + 1]
+            )
+
+        waiting = {}
+        for j in range(ROW_TILES):
+            banks = transposes(nc, psum_t, g_nat[:, j, :], ident)
+            sum_of_squares(g_nat[:, j, :], g_sq[:, j : j + 1])
+            waiting[j] = regroup(nc.vector.tensor_copy, stage, banks)
+            if j >= 1:
+                quantise_classes(j - 1, waiting[j - 1])
+        ready = {}
+        for i in range(AHEAD):
+            banks = transposes(nc, psum_t, x_nat[:, i, :], ident)
+            ready[i] = regroup(nc.vector.tensor_copy, stage, banks)
+            if i == 0:
+                quantise_classes(ROW_TILES - 1, waiting[ROW_TILES - 1])
+            else:
+                quantise_rows(i - 1, ready[i - 1])
+        quantise_rows(AHEAD - 1, ready[AHEAD - 1])
+        dots = {0: products(0)}
+
+        nc.vector.tensor_scalar_mul(out=g_half[:], in0=g_sq[:], scalar1=0.5)
+        nc.vector.tensor_scalar_max(out=g_safe[:], in0=g_sq[:], scalar1=TINY_SQ)
+        nc.scalar.activation(out=g_rough[:], in_=g_safe[:], func=ACT.Sqrt)
+        for i in range(AHEAD):
+            row_norms(i)
+        g_inv = newton_inverse_root(nc, small, g_safe, g_rough, "g")
+        g_half_all = spread_over_partitions(nc, psum_t, keep, g_half, ident, "g_half")
+        g_inv_all = spread_over_partitions(nc, psum_t, keep, g_inv, ident, "g_inv")
+
+        for i in range(ROW_TILES):
+            later = i + AHEAD
+            if later < ROW_TILES:
+                banks = transposes(nc, psum_t, x_nat[:, later, :], ident)
+            if i + 1 < ROW_TILES:
+                dots[i + 1] = products(i + 1)
+            if i >= 1:
+                nearest_distance(i - 1)
+            if later < ROW_TILES:
+                ready[later] = regroup(nc.scalar.copy, stage, banks)
+                row_norms(later)
+            cosine_and_distance(i, dots[i])
+            if i >= 1:
+                window(i - 1)
+                root(i - 1)
+            clamp_and_least(i)
+            if later < ROW_TILES:
+                quantise_rows(later, ready[later])
+        last = ROW_TILES - 1
+        nc.vector.tensor_scalar_max(out=x_safe[:], in0=x_sq[:], scalar1=TINY_SQ)
+        nearest_distance(last)
+        nc.scalar.activation(out=x_rough[:], in_=x_safe[:], func=ACT.Sqrt)
+        window(last)
+        root(last)
+
+        x_inv = newton_inverse_root(nc, small, x_safe, x_rough, "x")
+        nc.vector.tensor_scalar_mul(out=minus_gamma[:], in0=x_inv[:], scalar1=-GAMMA)
+        nc.vector.tensor_scalar_mul(out=minus_step[:], in0=step[:], scalar1=-1.0)
+
+        def scale_and_top(i):
+            nc.vector.tensor_scalar(
+                out=cosine[:, i, :], in0=cosine[:, i, :], scalar1=minus_gamma[:, i : i + 1],
+                scalar2=None, op0=ALU.mult, op1=ALU.min, accum_out=minus_top[:, i : i + 1],
+            )
+
+        scale_and_top(0)
+        for i in range(ROW_TILES):
+            col = slice(i, i + 1)
+            if i + 1 < ROW_TILES:
+                scale_and_top(i + 1)
+            nc.scalar.activation(
+                out=cosine[:, i, :], in_=cosine[:, i, :], func=ACT.Exp, scale=-1.0,
+                bias=minus_top[:, col], accum_out=sum_cos[:, col],
             )
             nc.scalar.activation(
-                out=cosine[:, i, :],
-                in_=cosine[:, i, :],
-                func=ACT.Exp,
-                scale=-1.0,
-                bias=minus_top[:, col],
-                accum_out=sum_cos[:, col],
-            )
-            nc.scalar.activation(
-                out=dist[:, i, :],
-                in_=dist[:, i, :],
-                func=ACT.Exp,
-                scale=minus_step[:, col],
-                bias=nearest[:, col],
-                accum_out=sum_dist[:, col],
+                out=dist[:, i, :], in_=dist[:, i, :], func=ACT.Exp, scale=minus_step[:, col],
+                bias=nearest[:, col], accum_out=sum_dist[:, col],
             )
             nc.vector.tensor_mul(out=sums[:, col], in0=sum_cos[:, col], in1=sum_dist[:, col])
             nc.vector.reciprocal(out=norm[:, col], in_=sums[:, col])
             nc.vector.scalar_tensor_tensor(
-                out=cosine[:, i, :],
-                in0=cosine[:, i, :],
-                scalar=norm[:, col],
-                in1=dist[:, i, :],
-                op0=ALU.mult,
-                op1=ALU.mult,
+                out=cosine[:, i, :], in0=cosine[:, i, :], scalar=norm[:, col],
+                in1=dist[:, i, :], op0=ALU.mult, op1=ALU.mult,
             )
             nc.sync.dma_start(out=out[P * i : P * (i + 1), :], in_=cosine[:, i, :])

@@ -20,12 +20,16 @@ N_MOVE = 512
 HALVES = C // N_MOVE
 AHEAD = 2
 
+LEAD = 3
+
 GAMMA = 100.0
 EPS = 1e-8
 TINY_SQ = 1e-30
 TINY_D2 = 1e-30
 CENTRE = 1.875
 WINDOW = 4.0
+
+ROOT_HALF = 0.5**0.5
 
 FLOPS = 2 * B * C * H
 
@@ -60,7 +64,7 @@ def newton_inverse_root(nc, small, safe, rough, name):
     nc.vector.tensor_mul(out=ratio[:], in0=guess[:], in1=guess[:])
     nc.vector.tensor_mul(out=ratio[:], in0=ratio[:], in1=safe[:])
     nc.vector.tensor_scalar(
-        out=ratio[:], in0=ratio[:], scalar1=-0.5, scalar2=1.5, op0=ALU.mult, op1=ALU.add
+        out=ratio[:], in0=ratio[:], scalar1=-1.0, scalar2=1.5, op0=ALU.mult, op1=ALU.add
     )
     inverse = small.tile([P, ROW_TILES], F32, name=name + "_inverse")
     nc.vector.tensor_mul(out=inverse[:], in0=guess[:], in1=ratio[:])
@@ -120,8 +124,8 @@ def tile_classifier_kernel(tc, X, grp, out):
         def stat(name):
             return small.tile([P, ROW_TILES], F32, name=name)
 
-        g_sq, g_half, g_safe, g_rough = stat("g_sq"), stat("g_half"), stat("g_safe"), stat("g_rough")
-        x_sq, x_half, x_cap = stat("x_sq"), stat("x_half"), stat("x_cap")
+        g_half, g_safe, g_rough = stat("g_half"), stat("g_safe"), stat("g_rough")
+        x_half, x_cap = stat("x_half"), stat("x_cap")
         x_safe, x_rough = stat("x_safe"), stat("x_rough")
         least, nearest, step, unit, zoom = (
             stat("least"), stat("nearest"), stat("step"), stat("unit"), stat("zoom"),
@@ -131,9 +135,11 @@ def tile_classifier_kernel(tc, X, grp, out):
         )
         sum_cos, sum_dist, sums, norm = stat("sum_cos"), stat("sum_dist"), stat("sums"), stat("norm")
 
-        def sum_of_squares(natural, total):
+        def half_sum_of_squares(natural, total):
             squares = scrap.tile([P, H], BF16, name="squares")
-            nc.scalar.activation(out=squares[:], in_=natural, func=ACT.Square, accum_out=total)
+            nc.scalar.activation(
+                out=squares[:], in_=natural, func=ACT.Square, scale=ROOT_HALF, accum_out=total
+            )
 
         def quantise_classes(j, grouped):
             cols = slice(P * j, P * (j + 1))
@@ -151,11 +157,10 @@ def tile_classifier_kernel(tc, X, grp, out):
 
         def row_norms(i):
             col = slice(i, i + 1)
-            sum_of_squares(x_nat[:, i, :], x_sq[:, col])
-            nc.scalar.mul(out=x_half[:, col], in_=x_sq[:, col], mul=0.5)
+            half_sum_of_squares(x_nat[:, i, :], x_half[:, col])
             nc.scalar.activation(
-                out=x_cap[:, col], in_=x_sq[:, col], func=ACT.Sqrt,
-                scale=1.0 / (EPS * EPS), bias=floor[:],
+                out=x_cap[:, col], in_=x_half[:, col], func=ACT.Sqrt,
+                scale=2.0 / (EPS * EPS), bias=floor[:],
             )
 
         def products(i):
@@ -177,14 +182,18 @@ def tile_classifier_kernel(tc, X, grp, out):
                 dots.append(dot)
             return dots
 
-        def cosine_and_distance(i, dots):
-            col = slice(i, i + 1)
+        def cosines(i, dots):
             for h in range(HALVES):
                 cols = slice(N_MOVE * h, N_MOVE * (h + 1))
                 nc.vector.scalar_tensor_tensor(
-                    out=cosine[:, i, cols], in0=g_inv_all[:, cols], scalar=x_cap[:, col],
+                    out=cosine[:, i, cols], in0=g_inv_all[:, cols], scalar=x_cap[:, i : i + 1],
                     in1=dots[h][:], op0=ALU.min, op1=ALU.mult,
                 )
+
+        def half_squared_distances(i, dots):
+            col = slice(i, i + 1)
+            for h in range(HALVES):
+                cols = slice(N_MOVE * h, N_MOVE * (h + 1))
                 nc.vector.scalar_tensor_tensor(
                     out=dist[:, i, cols], in0=g_half_all[:, cols], scalar=x_half[:, col],
                     in1=dots[h][:], op0=ALU.add, op1=ALU.subtract,
@@ -220,7 +229,7 @@ def tile_classifier_kernel(tc, X, grp, out):
         waiting = {}
         for j in range(ROW_TILES):
             banks = transposes(nc, psum_t, g_nat[:, j, :], ident)
-            sum_of_squares(g_nat[:, j, :], g_sq[:, j : j + 1])
+            half_sum_of_squares(g_nat[:, j, :], g_half[:, j : j + 1])
             waiting[j] = regroup(nc.vector.tensor_copy, stage, banks)
             if j >= 1:
                 quantise_classes(j - 1, waiting[j - 1])
@@ -235,11 +244,9 @@ def tile_classifier_kernel(tc, X, grp, out):
         quantise_rows(AHEAD - 1, ready[AHEAD - 1])
         dots = {0: products(0)}
 
-        nc.vector.tensor_scalar_mul(out=g_half[:], in0=g_sq[:], scalar1=0.5)
-        nc.vector.tensor_scalar_max(out=g_safe[:], in0=g_sq[:], scalar1=TINY_SQ)
-        nc.scalar.activation(out=g_rough[:], in_=g_safe[:], func=ACT.Sqrt)
-        for i in range(AHEAD):
-            row_norms(i)
+        nc.vector.tensor_scalar_max(out=g_safe[:], in0=g_half[:], scalar1=TINY_SQ)
+        nc.scalar.activation(out=g_rough[:], in_=g_safe[:], func=ACT.Sqrt, scale=2.0)
+        row_norms(0)
         g_inv = newton_inverse_root(nc, small, g_safe, g_rough, "g")
         g_half_all = spread_over_partitions(nc, psum_t, keep, g_half, ident, "g_half")
         g_inv_all = spread_over_partitions(nc, psum_t, keep, g_inv, ident, "g_inv")
@@ -254,18 +261,20 @@ def tile_classifier_kernel(tc, X, grp, out):
                 nearest_distance(i - 1)
             if later < ROW_TILES:
                 ready[later] = regroup(nc.scalar.copy, stage, banks)
-                row_norms(later)
-            cosine_and_distance(i, dots[i])
+            if i + 1 < ROW_TILES:
+                row_norms(i + 1)
+            half_squared_distances(i, dots[i])
+            clamp_and_least(i)
             if i >= 1:
                 window(i - 1)
                 root(i - 1)
-            clamp_and_least(i)
             if later < ROW_TILES:
+                cosines(i, dots[i])
                 quantise_rows(later, ready[later])
         last = ROW_TILES - 1
-        nc.vector.tensor_scalar_max(out=x_safe[:], in0=x_sq[:], scalar1=TINY_SQ)
+        nc.vector.tensor_scalar_max(out=x_safe[:], in0=x_half[:], scalar1=TINY_SQ)
         nearest_distance(last)
-        nc.scalar.activation(out=x_rough[:], in_=x_safe[:], func=ACT.Sqrt)
+        nc.scalar.activation(out=x_rough[:], in_=x_safe[:], func=ACT.Sqrt, scale=2.0)
         window(last)
         root(last)
 
@@ -280,10 +289,14 @@ def tile_classifier_kernel(tc, X, grp, out):
             )
 
         scale_and_top(0)
+        for i in range(ROW_TILES - AHEAD, ROW_TILES):
+            cosines(i, dots[i])
+        for i in range(1, LEAD):
+            scale_and_top(i)
         for i in range(ROW_TILES):
             col = slice(i, i + 1)
-            if i + 1 < ROW_TILES:
-                scale_and_top(i + 1)
+            if i + LEAD < ROW_TILES:
+                scale_and_top(i + LEAD)
             nc.scalar.activation(
                 out=cosine[:, i, :], in_=cosine[:, i, :], func=ACT.Exp, scale=-1.0,
                 bias=minus_top[:, col], accum_out=sum_cos[:, col],

@@ -96,7 +96,6 @@ def tile_classifier_kernel(tc, X, grp, out):
         scrap = ctx.enter_context(tc.tile_pool(name="scrap", bufs=2))
         psum_t = ctx.enter_context(tc.psum_pool(name="psum_t", bufs=4))
         psum_d = ctx.enter_context(tc.psum_pool(name="psum_d", bufs=4))
-        ctx.enter_context(tc.manual_schedule())
 
         g_nat = keep.tile([P, ROW_TILES, H], BF16, name="g_nat")
         x_nat = keep.tile([P, ROW_TILES, H], BF16, name="x_nat")

@@ -18,8 +18,13 @@ K_PASS = 4 * P
 PASSES = H // K_PASS
 N_MOVE = 512
 HALVES = C // N_MOVE
-AHEAD = 2
 
+CLASSES_ON_TENSOR = (1, 2, 4, 5)
+CLASSES_COPIED_BY_SCALAR = (2, 4, 5)
+ROWS_ON_TENSOR = (2, 4)
+SQUARES_AHEAD = 2
+AHEAD = 2
+HELD = 3
 LEAD = 3
 
 GAMMA = 100.0
@@ -34,59 +39,6 @@ ROOT_HALF = 0.5**0.5
 FLOPS = 2 * B * C * H
 
 
-def transposes(nc, psum, natural, ident):
-    words = natural.bitcast(F32)
-    banks = []
-    for bank in range(2):
-        flipped = psum.tile([P, 4, P], F32, name="flipped", tag="flipped")
-        for w in range(4):
-            first = (4 * bank + w) * P
-            nc.tensor.transpose(flipped[:, w, :], words[:, first : first + P], ident[:])
-        banks.append(flipped)
-    return banks
-
-
-def regroup(copy, stage, banks):
-    grouped = stage.tile([P, 4 * PASSES * P], BF16, align_bytes=64, name="grouped")
-    grouped_words = grouped[:].bitcast(F32).rearrange("p (g r u) -> p g r u", g=PASSES, u=2)
-    for bank in range(2):
-        copy(
-            out=grouped_words[:, 2 * bank : 2 * bank + 2],
-            in_=banks[bank][:].rearrange("p (g u) r -> p g r u", u=2),
-        )
-    return grouped
-
-
-def newton_inverse_root(nc, small, safe, rough, name):
-    guess = small.tile([P, ROW_TILES], F32, name=name + "_guess")
-    nc.vector.reciprocal(out=guess[:], in_=rough[:])
-    ratio = small.tile([P, ROW_TILES], F32, name=name + "_ratio")
-    nc.vector.tensor_mul(out=ratio[:], in0=guess[:], in1=guess[:])
-    nc.vector.tensor_mul(out=ratio[:], in0=ratio[:], in1=safe[:])
-    nc.vector.tensor_scalar(
-        out=ratio[:], in0=ratio[:], scalar1=-1.0, scalar2=1.5, op0=ALU.mult, op1=ALU.add
-    )
-    inverse = small.tile([P, ROW_TILES], F32, name=name + "_inverse")
-    nc.vector.tensor_mul(out=inverse[:], in0=guess[:], in1=ratio[:])
-    return inverse
-
-
-def spread_over_partitions(nc, psum, keep, per_class, ident, name):
-    spread = keep.tile([P, C], F32, name=name + "_spread")
-    for h in range(HALVES):
-        flipped = psum.tile([P, 4, P], F32, name="flipped", tag="flipped")
-        for w in range(4):
-            j = 4 * h + w
-            nc.tensor.transpose(
-                flipped[:, w, :], per_class[:, j : j + 1].to_broadcast([P, P]), ident[:]
-            )
-        nc.vector.tensor_copy(
-            out=spread[:, N_MOVE * h : N_MOVE * (h + 1)],
-            in_=flipped[:].rearrange("p w c -> p (w c)"),
-        )
-    return spread
-
-
 def tile_classifier_kernel(tc, X, grp, out):
     nc = tc.nc
     with ExitStack() as ctx:
@@ -94,8 +46,8 @@ def tile_classifier_kernel(tc, X, grp, out):
         small = ctx.enter_context(tc.tile_pool(name="small", bufs=1))
         stage = ctx.enter_context(tc.tile_pool(name="stage", bufs=3))
         scrap = ctx.enter_context(tc.tile_pool(name="scrap", bufs=2))
-        psum_t = ctx.enter_context(tc.psum_pool(name="psum_t", bufs=4))
-        psum_d = ctx.enter_context(tc.psum_pool(name="psum_d", bufs=4))
+        psum = ctx.enter_context(tc.psum_pool(name="psum", bufs=8))
+        ctx.enter_context(tc.manual_schedule())
 
         g_nat = keep.tile([P, ROW_TILES, H], BF16, name="g_nat")
         x_nat = keep.tile([P, ROW_TILES, H], BF16, name="x_nat")
@@ -109,9 +61,11 @@ def tile_classifier_kernel(tc, X, grp, out):
 
         warm = small.tile([P, 1], F32, name="warm")
         nc.vector.memset(warm[:], 1.0)
-        floor = small.tile([P, 1], F32, name="floor")
-        nc.vector.memset(floor[:], TINY_SQ / (EPS * EPS))
         nc.scalar.activation(out=warm[:], in_=warm[:], func=ACT.Sqrt)
+        power = small.tile([P, 4, ROW_TILES], F32, name="power")
+        for k, exponent in enumerate((0.5, -0.5, -1.0, -2.0)):
+            nc.vector.memset(power[:, k, :], exponent)
+        ROOT, INVERSE_ROOT, INVERSE, INVERSE_SQUARE = (power[:, k, :] for k in range(4))
 
         g_codes = keep.tile([P, PASSES, C], U32, align_bytes=64, name="g_codes")
         g_scales = keep.tile([P, PASSES, C], U8, align_bytes=64, name="g_scales")
@@ -119,54 +73,50 @@ def tile_classifier_kernel(tc, X, grp, out):
         x_scales = keep.tile([P, ROW_TILES, PASSES * P], U8, align_bytes=64, name="x_scales")
         cosine = keep.tile([P, ROW_TILES, C], F32, name="cosine")
         dist = keep.tile([P, ROW_TILES, C], F32, name="dist")
+        g_half_all = keep.tile([P, C], F32, name="g_half_all")
+        g_inv_all = keep.tile([P, C], F32, name="g_inv_all")
 
         def stat(name):
             return small.tile([P, ROW_TILES], F32, name=name)
 
-        g_half, g_safe, g_rough = stat("g_half"), stat("g_safe"), stat("g_rough")
-        x_half, x_cap = stat("x_half"), stat("x_cap")
-        x_safe, x_rough = stat("x_safe"), stat("x_rough")
-        least, nearest, step, unit, zoom = (
-            stat("least"), stat("nearest"), stat("step"), stat("unit"), stat("zoom"),
+        g_half, g_square, g_inv = stat("g_half"), stat("g_square"), stat("g_inv")
+        x_half, x_norm, x_cap = stat("x_half"), stat("x_norm"), stat("x_cap")
+        x_square, x_inv, gamma_inv, minus_gamma_inv = (
+            stat("x_square"), stat("x_inv"), stat("gamma_inv"), stat("minus_gamma_inv"),
         )
-        minus_gamma, minus_step, minus_top = (
-            stat("minus_gamma"), stat("minus_step"), stat("minus_top"),
+        least, root_least, nearest, minus_step, unit_root, zoom = (
+            stat("least"), stat("root_least"), stat("nearest"), stat("minus_step"),
+            stat("unit_root"), stat("zoom"),
         )
+        top, minus_top = stat("top"), stat("minus_top")
         sum_cos, sum_dist, sums, norm = stat("sum_cos"), stat("sum_dist"), stat("sums"), stat("norm")
+        last_sums, last_norm = stat("last_sums"), stat("last_norm")
 
-        def half_sum_of_squares(natural, total):
-            squares = scrap.tile([P, H], BF16, name="squares")
-            nc.scalar.activation(
-                out=squares[:], in_=natural, func=ACT.Square, scale=ROOT_HALF, accum_out=total
-            )
+        def transposes(natural):
+            words = natural.bitcast(F32)
+            banks = []
+            for bank in range(2):
+                flipped = psum.tile([P, 4, P], F32, name="bank", tag="bank")
+                for w in range(4):
+                    first = (4 * bank + w) * P
+                    nc.tensor.transpose(flipped[:, w, :], words[:, first : first + P], ident[:])
+                banks.append(flipped)
+            return banks
 
-        def quantise_classes(j, grouped):
-            cols = slice(P * j, P * (j + 1))
+        def squares_on_tensor(bank, grouped):
+            columns = grouped.rearrange("p g (r t) -> p g r t", t=4)
             for g in range(PASSES):
-                nc.vector.quantize_mx(
-                    out=g_codes[:, g, cols].bitcast(FP8X4),
-                    scales=g_scales[:, g, cols],
-                    in_=grouped[:, K_PASS * g : K_PASS * (g + 1)],
-                )
-
-        def quantise_rows(i, grouped):
-            nc.vector.quantize_mx(
-                out=x_codes[:, i, :].bitcast(FP8X4), scales=x_scales[:, i, :], in_=grouped[:]
-            )
-
-        def row_norms(i):
-            col = slice(i, i + 1)
-            half_sum_of_squares(x_nat[:, i, :], x_half[:, col])
-            nc.scalar.activation(
-                out=x_cap[:, col], in_=x_half[:, col], func=ACT.Sqrt,
-                scale=2.0 / (EPS * EPS), bias=floor[:],
-            )
+                for t in range(4):
+                    nc.tensor.matmul(
+                        out=bank, lhsT=columns[:, g, :, t], rhs=columns[:, g, :, t],
+                        start=(g == 0 and t == 0), stop=(g == PASSES - 1 and t == 3),
+                    )
 
         def products(i):
             dots = []
             for h in range(HALVES):
                 cols = slice(N_MOVE * h, N_MOVE * (h + 1))
-                dot = psum_d.tile([P, N_MOVE], F32, name="dot")
+                dot = psum.tile([P, N_MOVE], F32, name="bank", tag="bank")
                 for g in range(PASSES):
                     rows = slice(P * g, P * (g + 1))
                     nc.tensor.matmul_mx(
@@ -181,20 +131,77 @@ def tile_classifier_kernel(tc, X, grp, out):
                 dots.append(dot)
             return dots
 
-        def cosines(i, dots):
-            for h in range(HALVES):
-                cols = slice(N_MOVE * h, N_MOVE * (h + 1))
-                nc.vector.scalar_tensor_tensor(
-                    out=cosine[:, i, cols], in0=g_inv_all[:, cols], scalar=x_cap[:, i : i + 1],
-                    in1=dots[h][:], op0=ALU.min, op1=ALU.mult,
+        def spread_on_tensor(per_class, h):
+            flipped = psum.tile([P, 4, P], F32, name="bank", tag="bank")
+            for w in range(4):
+                j = 4 * h + w
+                nc.tensor.transpose(
+                    flipped[:, w, :], per_class[:, j : j + 1].to_broadcast([P, P]), ident[:]
+                )
+            return flipped
+
+        def regroup(copy, grouped, bank, flipped):
+            copy(
+                out=grouped.bitcast(F32)[:, 2 * bank : 2 * bank + 2, :].rearrange(
+                    "p g (r u) -> p g r u", u=2
+                ),
+                in_=flipped[:].rearrange("p (g u) r -> p g r u", u=2),
+            )
+
+        def spread_out(copy, spread, h, flipped):
+            copy(
+                out=spread[:, N_MOVE * h : N_MOVE * (h + 1)],
+                in_=flipped[:].rearrange("p w c -> p (w c)"),
+            )
+
+        def half_sum_of_squares(natural, total):
+            squares = scrap.tile([P, H], BF16, name="squares")
+            nc.scalar.activation(
+                out=squares[:], in_=natural, func=ACT.Square, scale=ROOT_HALF, accum_out=total
+            )
+
+        def root(i):
+            nc.scalar.activation(
+                out=dist[:, i, :], in_=dist[:, i, :], func=ACT.Sqrt, scale=zoom[:, i : i + 1]
+            )
+
+        def exponentials(i):
+            col = slice(i, i + 1)
+            nc.scalar.activation(
+                out=cosine[:, i, :], in_=cosine[:, i, :], func=ACT.Exp, scale=gamma_inv[:, col],
+                bias=minus_top[:, col], accum_out=sum_cos[:, col],
+            )
+            nc.scalar.activation(
+                out=dist[:, i, :], in_=dist[:, i, :], func=ACT.Exp, scale=minus_step[:, col],
+                bias=nearest[:, col], accum_out=sum_dist[:, col],
+            )
+
+        def half_diagonal(bank, total):
+            masked = scrap.tile([P, P], F32, name="masked")
+            nc.vector.scalar_tensor_tensor(
+                out=masked[:], in0=bank, scalar=0.5, in1=ident[:],
+                op0=ALU.mult, op1=ALU.mult, accum_out=total,
+            )
+
+        def quantise_class_pair(pair, grouped):
+            cols = slice(2 * P * pair, 2 * P * (pair + 1))
+            for g in range(PASSES):
+                nc.vector.quantize_mx(
+                    out=g_codes[:, g, cols].bitcast(FP8X4), scales=g_scales[:, g, cols],
+                    in_=grouped[:, g, :],
                 )
 
+        def quantise_rows(i, grouped):
+            nc.vector.quantize_mx(
+                out=x_codes[:, i, :].bitcast(FP8X4), scales=x_scales[:, i, :],
+                in_=grouped.rearrange("p g r -> p (g r)"),
+            )
+
         def half_squared_distances(i, dots):
-            col = slice(i, i + 1)
             for h in range(HALVES):
                 cols = slice(N_MOVE * h, N_MOVE * (h + 1))
                 nc.vector.scalar_tensor_tensor(
-                    out=dist[:, i, cols], in0=g_half_all[:, cols], scalar=x_half[:, col],
+                    out=dist[:, i, cols], in0=g_half_all[:, cols], scalar=x_half[:, i : i + 1],
                     in1=dots[h][:], op0=ALU.add, op1=ALU.subtract,
                 )
 
@@ -204,110 +211,214 @@ def tile_classifier_kernel(tc, X, grp, out):
                 op0=ALU.max, op1=ALU.min, accum_out=least[:, i : i + 1],
             )
 
-        def nearest_distance(i):
-            col = slice(i, i + 1)
-            nc.scalar.activation(out=nearest[:, col], in_=least[:, col], func=ACT.Sqrt, scale=2.0)
+        def cosines(i, dots):
+            for h in range(HALVES):
+                cols = slice(N_MOVE * h, N_MOVE * (h + 1))
+                nc.vector.scalar_tensor_tensor(
+                    out=cosine[:, i, cols], in0=g_inv_all[:, cols], scalar=x_cap[:, i : i + 1],
+                    in1=dots[h][:], op0=ALU.min, op1=ALU.mult,
+                )
 
-        def window(i):
-            col = slice(i, i + 1)
-            nc.vector.tensor_scalar(
-                out=step[:, col], in0=nearest[:, col], scalar1=WINDOW, scalar2=CENTRE**-0.5,
-                op0=ALU.add, op1=ALU.mult,
-            )
-            nc.vector.tensor_scalar(
-                out=unit[:, col], in0=step[:, col], scalar1=0.5, scalar2=step[:, col],
-                op0=ALU.mult, op1=ALU.mult,
-            )
-            nc.vector.reciprocal(out=zoom[:, col], in_=unit[:, col])
-
-        def root(i):
-            nc.scalar.activation(
-                out=dist[:, i, :], in_=dist[:, i, :], func=ACT.Sqrt, scale=zoom[:, i : i + 1]
+        def largest_cosine(i):
+            nc.vector.tensor_reduce(
+                out=top[:, i : i + 1], in_=cosine[:, i, :], axis=mybir.AxisListType.X, op=ALU.max
             )
 
-        waiting = {}
-        for j in range(ROW_TILES):
-            banks = transposes(nc, psum_t, g_nat[:, j, :], ident)
-            half_sum_of_squares(g_nat[:, j, :], g_half[:, j : j + 1])
-            waiting[j] = regroup(nc.vector.tensor_copy, stage, banks)
-            if j >= 1:
-                quantise_classes(j - 1, waiting[j - 1])
-        ready = {}
-        for i in range(AHEAD):
-            banks = transposes(nc, psum_t, x_nat[:, i, :], ident)
-            ready[i] = regroup(nc.vector.tensor_copy, stage, banks)
-            if i == 0:
-                quantise_classes(ROW_TILES - 1, waiting[ROW_TILES - 1])
-            else:
-                quantise_rows(i - 1, ready[i - 1])
-        quantise_rows(AHEAD - 1, ready[AHEAD - 1])
-        dots = {0: products(0)}
-
-        nc.vector.tensor_scalar_max(out=g_safe[:], in0=g_half[:], scalar1=TINY_SQ)
-        nc.scalar.activation(out=g_rough[:], in_=g_safe[:], func=ACT.Sqrt, scale=2.0)
-        row_norms(0)
-        g_inv = newton_inverse_root(nc, small, g_safe, g_rough, "g")
-        g_half_all = spread_over_partitions(nc, psum_t, keep, g_half, ident, "g_half")
-        g_inv_all = spread_over_partitions(nc, psum_t, keep, g_inv, ident, "g_inv")
-
-        for i in range(ROW_TILES):
-            later = i + AHEAD
-            if later < ROW_TILES:
-                banks = transposes(nc, psum_t, x_nat[:, later, :], ident)
-            if i + 1 < ROW_TILES:
-                dots[i + 1] = products(i + 1)
-            if i >= 1:
-                nearest_distance(i - 1)
-            if later < ROW_TILES:
-                ready[later] = regroup(nc.scalar.copy, stage, banks)
-            if i + 1 < ROW_TILES:
-                row_norms(i + 1)
-            half_squared_distances(i, dots[i])
-            clamp_and_least(i)
-            if i >= 1:
-                window(i - 1)
-                root(i - 1)
-            if later < ROW_TILES:
-                cosines(i, dots[i])
-                quantise_rows(later, ready[later])
-        last = ROW_TILES - 1
-        nc.vector.tensor_scalar_max(out=x_safe[:], in0=x_half[:], scalar1=TINY_SQ)
-        nearest_distance(last)
-        nc.scalar.activation(out=x_rough[:], in_=x_safe[:], func=ACT.Sqrt, scale=2.0)
-        window(last)
-        root(last)
-
-        x_inv = newton_inverse_root(nc, small, x_safe, x_rough, "x")
-        nc.vector.tensor_scalar_mul(out=minus_gamma[:], in0=x_inv[:], scalar1=-GAMMA)
-        nc.vector.tensor_scalar_mul(out=minus_step[:], in0=step[:], scalar1=-1.0)
-
-        def scale_and_top(i):
-            nc.vector.tensor_scalar(
-                out=cosine[:, i, :], in0=cosine[:, i, :], scalar1=minus_gamma[:, i : i + 1],
-                scalar2=None, op0=ALU.mult, op1=ALU.min, accum_out=minus_top[:, i : i + 1],
-            )
-
-        scale_and_top(0)
-        for i in range(ROW_TILES - AHEAD, ROW_TILES):
-            cosines(i, dots[i])
-        for i in range(1, LEAD):
-            scale_and_top(i)
-        for i in range(ROW_TILES):
-            col = slice(i, i + 1)
-            if i + LEAD < ROW_TILES:
-                scale_and_top(i + LEAD)
-            nc.scalar.activation(
-                out=cosine[:, i, :], in_=cosine[:, i, :], func=ACT.Exp, scale=-1.0,
-                bias=minus_top[:, col], accum_out=sum_cos[:, col],
-            )
-            nc.scalar.activation(
-                out=dist[:, i, :], in_=dist[:, i, :], func=ACT.Exp, scale=minus_step[:, col],
-                bias=nearest[:, col], accum_out=sum_dist[:, col],
-            )
-            nc.vector.tensor_mul(out=sums[:, col], in0=sum_cos[:, col], in1=sum_dist[:, col])
-            nc.vector.reciprocal(out=norm[:, col], in_=sums[:, col])
+        def weigh_and_store(i, factor):
             nc.vector.scalar_tensor_tensor(
-                out=cosine[:, i, :], in0=cosine[:, i, :], scalar=norm[:, col],
+                out=cosine[:, i, :], in0=cosine[:, i, :], scalar=factor,
                 in1=dist[:, i, :], op0=ALU.mult, op1=ALU.mult,
             )
             nc.sync.dma_start(out=out[P * i : P * (i + 1), :], in_=cosine[:, i, :])
+
+        def class_norms(h):
+            tiles = slice(4 * h, 4 * (h + 1))
+            nc.gpsimd.tensor_scalar(
+                out=g_square[:, tiles], in0=g_half[:, tiles], scalar1=TINY_SQ, scalar2=2.0,
+                op0=ALU.max, op1=ALU.mult,
+            )
+            nc.gpsimd.tensor_tensor(
+                out=g_inv[:, tiles], in0=g_square[:, tiles], in1=INVERSE_ROOT[:, tiles], op=ALU.pow
+            )
+
+        def row_norms(h):
+            tiles = slice(4 * h, 4 * (h + 1))
+            nc.gpsimd.tensor_scalar(
+                out=x_square[:, tiles], in0=x_half[:, tiles], scalar1=TINY_SQ, scalar2=2.0,
+                op0=ALU.max, op1=ALU.mult,
+            )
+            nc.gpsimd.tensor_tensor(
+                out=x_inv[:, tiles], in0=x_square[:, tiles], in1=INVERSE_ROOT[:, tiles], op=ALU.pow
+            )
+            for gamma, scaled in ((GAMMA, gamma_inv), (-GAMMA, minus_gamma_inv)):
+                nc.gpsimd.tensor_scalar(
+                    out=scaled[:, tiles], in0=x_inv[:, tiles], scalar1=gamma, scalar2=1.0,
+                    op0=ALU.mult, op1=ALU.mult,
+                )
+
+        def row_cap(i):
+            col = slice(i, i + 1)
+            nc.gpsimd.tensor_tensor(
+                out=x_norm[:, col], in0=x_half[:, col], in1=ROOT[:, col], op=ALU.pow
+            )
+            nc.gpsimd.tensor_scalar(
+                out=x_cap[:, col], in0=x_norm[:, col], scalar1=2.0**0.5 / EPS, scalar2=1.0,
+                op0=ALU.mult, op1=ALU.mult,
+            )
+
+        def window(i):
+            col = slice(i, i + 1)
+            nc.gpsimd.tensor_tensor(
+                out=root_least[:, col], in0=least[:, col], in1=ROOT[:, col], op=ALU.pow
+            )
+            nc.gpsimd.tensor_scalar(
+                out=unit_root[:, col], in0=root_least[:, col],
+                scalar1=CENTRE**-0.5, scalar2=WINDOW * (0.5 / CENTRE) ** 0.5,
+                op0=ALU.mult, op1=ALU.add,
+            )
+            nc.gpsimd.tensor_tensor(
+                out=zoom[:, col], in0=unit_root[:, col], in1=INVERSE_SQUARE[:, col], op=ALU.pow
+            )
+            nc.gpsimd.tensor_scalar(
+                out=nearest[:, col], in0=root_least[:, col], scalar1=2.0**0.5, scalar2=1.0,
+                op0=ALU.mult, op1=ALU.mult,
+            )
+            nc.gpsimd.tensor_scalar(
+                out=minus_step[:, col], in0=unit_root[:, col], scalar1=-(2.0**0.5), scalar2=1.0,
+                op0=ALU.mult, op1=ALU.mult,
+            )
+
+        def exponent_shift(i):
+            col = slice(i, i + 1)
+            nc.gpsimd.tensor_tensor(
+                out=minus_top[:, col], in0=top[:, col], in1=minus_gamma_inv[:, col], op=ALU.mult
+            )
+
+        def normaliser(i):
+            col = slice(i, i + 1)
+            if i + 1 < ROW_TILES:
+                nc.gpsimd.tensor_tensor(
+                    out=sums[:, col], in0=sum_cos[:, col], in1=sum_dist[:, col], op=ALU.mult
+                )
+                nc.gpsimd.tensor_tensor(
+                    out=norm[:, col], in0=sums[:, col], in1=INVERSE[:, col], op=ALU.pow
+                )
+                return norm[:, col]
+            nc.vector.tensor_tensor(
+                out=last_sums[:, col], in0=sum_cos[:, col], in1=sum_dist[:, col], op=ALU.mult
+            )
+            nc.vector.reciprocal(out=last_norm[:, col], in_=last_sums[:, col])
+            return last_norm[:, col]
+
+        def square_row(i):
+            half_sum_of_squares(x_nat[:, i, :], x_half[:, i : i + 1])
+            row_cap(i)
+
+        grouped_pairs = []
+        flipped = {}
+        class_square = {}
+
+        def class_slot(j):
+            return grouped_pairs[j // 2][:, :, K_PASS * (j % 2) : K_PASS * (j % 2 + 1)]
+
+        ready = {}
+
+        def copies(engine_copy, grouped, banks):
+            for bank in range(2):
+                regroup(engine_copy, grouped, bank, banks[bank])
+
+        for j in range(ROW_TILES + AHEAD):
+            if j < ROW_TILES:
+                flipped[j] = transposes(g_nat[:, j, :])
+                if j % 2 == 0:
+                    grouped = stage.tile(
+                        [P, PASSES, 2 * K_PASS], BF16, align_bytes=64, name="grouped_pair"
+                    )
+                    grouped_pairs.append(grouped)
+            else:
+                flipped[j] = transposes(x_nat[:, j - ROW_TILES, :])
+            if j - 2 in CLASSES_ON_TENSOR:
+                class_square[j - 2] = psum.tile([P, N_MOVE], F32, name="bank", tag="bank")
+                squares_on_tensor(class_square[j - 2][:, :P], class_slot(j - 2))
+            if j < ROW_TILES:
+                if j in CLASSES_COPIED_BY_SCALAR:
+                    copies(nc.scalar.copy, class_slot(j), flipped[j])
+                else:
+                    copies(nc.vector.tensor_copy, class_slot(j), flipped[j])
+                if j not in CLASSES_ON_TENSOR:
+                    half_sum_of_squares(g_nat[:, j, :], g_half[:, j : j + 1])
+            else:
+                i = j - ROW_TILES
+                ready[i] = stage.tile([P, PASSES, K_PASS], BF16, align_bytes=64, name="grouped", bufs=4)
+                copies(nc.scalar.copy if i == 0 else nc.vector.tensor_copy, ready[i][:], flipped[j])
+                half_sum_of_squares(x_nat[:, i, :], x_half[:, i : i + 1])
+                row_cap(i)
+            if j >= 2 and j % 2 == 0:
+                quantise_class_pair(j // 2 - 1, grouped_pairs[j // 2 - 1][:])
+            if j - 3 in CLASSES_ON_TENSOR:
+                half_diagonal(class_square[j - 3][:, :P], g_half[:, j - 3 : j - 2])
+            if j in (5, ROW_TILES):
+                class_norms(0 if j == 5 else 1)
+        for i in range(AHEAD):
+            quantise_rows(i, ready[i][:])
+        spread_out(nc.vector.tensor_copy, g_half_all, 0, spread_on_tensor(g_half, 0))
+        half_bank = spread_on_tensor(g_half, 1)
+        inverse_banks = [spread_on_tensor(g_inv, 0)]
+        spread_out(nc.vector.tensor_copy, g_half_all, 1, half_bank)
+        spread_out(nc.scalar.copy, g_inv_all, 0, inverse_banks[0])
+        dots = {0: products(0)}
+        inverse_banks.append(spread_on_tensor(g_inv, 1))
+
+        row_square = {}
+        for i in range(ROW_TILES):
+            later = i + AHEAD
+            if later < ROW_TILES:
+                flipped[later] = transposes(x_nat[:, later, :])
+            if i + 1 < ROW_TILES:
+                dots[i + 1] = products(i + 1)
+            if i + 1 in ROWS_ON_TENSOR:
+                row_square[i + 1] = psum.tile([P, 4, P], F32, name="bank", tag="bank")
+                squares_on_tensor(row_square[i + 1][:, 0, :], ready[i + 1][:])
+            half_squared_distances(i, dots[i])
+            clamp_and_least(i)
+            window(i)
+            if i == 0:
+                spread_out(nc.vector.tensor_copy, g_inv_all, 1, inverse_banks[1])
+            if i < ROW_TILES - HELD:
+                cosines(i, dots[i])
+            if AHEAD <= i + SQUARES_AHEAD < ROW_TILES and i + SQUARES_AHEAD not in ROWS_ON_TENSOR:
+                square_row(i + SQUARES_AHEAD)
+            if i == 0:
+                for k in range(AHEAD, SQUARES_AHEAD):
+                    square_row(k)
+            if later < ROW_TILES:
+                ready[later] = stage.tile([P, PASSES, K_PASS], BF16, align_bytes=64, name="grouped", bufs=4)
+                copies(nc.scalar.copy, ready[later][:], flipped[later])
+            if i >= 1:
+                root(i - 1)
+            if i + 1 in ROWS_ON_TENSOR:
+                half_diagonal(row_square[i + 1][:, 0, :], x_half[:, i + 1 : i + 2])
+                row_cap(i + 1)
+            if later < ROW_TILES:
+                quantise_rows(later, ready[later][:])
+            if i == 3:
+                row_norms(0)
+        row_norms(1)
+        for i in range(LEAD):
+            largest_cosine(i)
+        root(ROW_TILES - 1)
+        for i in range(LEAD):
+            exponent_shift(i)
+
+        factors = {}
+        for i in range(ROW_TILES):
+            exponentials(i)
+            if i < HELD:
+                cosines(ROW_TILES - HELD + i, dots[ROW_TILES - HELD + i])
+            if i + LEAD < ROW_TILES:
+                largest_cosine(i + LEAD)
+                exponent_shift(i + LEAD)
+            factors[i] = normaliser(i)
+            if i >= 1:
+                weigh_and_store(i - 1, factors[i - 1])
+        weigh_and_store(ROW_TILES - 1, factors[ROW_TILES - 1])

@@ -62,10 +62,13 @@ def tile_classifier_kernel(tc, X, grp, out):
         warm = small.tile([P, 1], F32, name="warm")
         nc.vector.memset(warm[:], 1.0)
         nc.scalar.activation(out=warm[:], in_=warm[:], func=ACT.Sqrt)
-        power = small.tile([P, 4, ROW_TILES], F32, name="power")
-        for k, exponent in enumerate((0.5, -0.5, -1.0, -2.0)):
-            nc.vector.memset(power[:, k, :], exponent)
-        ROOT, INVERSE_ROOT, INVERSE, INVERSE_SQUARE = (power[:, k, :] for k in range(4))
+        cap_floor = small.tile([P, 1], F32, name="cap_floor")
+        nc.vector.memset(cap_floor[:], TINY_SQ / (EPS * EPS))
+        unit_shift = small.tile([P, 1], F32, name="unit_shift")
+        nc.vector.memset(unit_shift[:], 1.0)
+        nc.vector.tensor_scalar_mul(
+            out=unit_shift[:], in0=unit_shift[:], scalar1=WINDOW * (0.5 / CENTRE) ** 0.5
+        )
 
         g_codes = keep.tile([P, PASSES, C], U32, align_bytes=64, name="g_codes")
         g_scales = keep.tile([P, PASSES, C], U8, align_bytes=64, name="g_scales")
@@ -79,18 +82,13 @@ def tile_classifier_kernel(tc, X, grp, out):
         def stat(name):
             return small.tile([P, ROW_TILES], F32, name=name)
 
-        g_half, g_square, g_inv = stat("g_half"), stat("g_square"), stat("g_inv")
-        x_half, x_norm, x_cap = stat("x_half"), stat("x_norm"), stat("x_cap")
-        x_square, x_inv, gamma_inv, minus_gamma_inv = (
-            stat("x_square"), stat("x_inv"), stat("gamma_inv"), stat("minus_gamma_inv"),
-        )
-        least, root_least, nearest, minus_step, unit_root, zoom = (
-            stat("least"), stat("root_least"), stat("nearest"), stat("minus_step"),
-            stat("unit_root"), stat("zoom"),
+        g_half, x_half, x_cap = stat("g_half"), stat("x_half"), stat("x_cap")
+        gamma_inv, minus_gamma_inv = stat("gamma_inv"), stat("minus_gamma_inv")
+        least, nearest, minus_step, unit, zoom = (
+            stat("least"), stat("nearest"), stat("minus_step"), stat("unit"), stat("zoom"),
         )
         top, minus_top = stat("top"), stat("minus_top")
         sum_cos, sum_dist, sums, norm = stat("sum_cos"), stat("sum_dist"), stat("sums"), stat("norm")
-        last_sums, last_norm = stat("last_sums"), stat("last_norm")
 
         def transposes(natural):
             words = natural.bitcast(F32)
@@ -131,12 +129,11 @@ def tile_classifier_kernel(tc, X, grp, out):
                 dots.append(dot)
             return dots
 
-        def spread_on_tensor(per_class, h):
+        def spread_on_tensor(per_class):
             flipped = psum.tile([P, 4, P], F32, name="bank", tag="bank")
             for w in range(4):
-                j = 4 * h + w
                 nc.tensor.transpose(
-                    flipped[:, w, :], per_class[:, j : j + 1].to_broadcast([P, P]), ident[:]
+                    flipped[:, w, :], per_class[:, w : w + 1].to_broadcast([P, P]), ident[:]
                 )
             return flipped
 
@@ -231,61 +228,62 @@ def tile_classifier_kernel(tc, X, grp, out):
             )
             nc.sync.dma_start(out=out[P * i : P * (i + 1), :], in_=cosine[:, i, :])
 
-        def class_norms(h):
-            tiles = slice(4 * h, 4 * (h + 1))
+        def rough_roots(half_squares, tiles, name):
+            width = tiles.stop - tiles.start
+            safe, rough, guess, ratio, inverse = (
+                small.tile([P, width], F32, name=name + part)
+                for part in ("_safe", "_rough", "_guess", "_ratio", "_inverse")
+            )
             nc.gpsimd.tensor_scalar(
-                out=g_square[:, tiles], in0=g_half[:, tiles], scalar1=TINY_SQ, scalar2=2.0,
+                out=safe[:], in0=half_squares[:, tiles], scalar1=TINY_SQ, scalar2=-1.0,
                 op0=ALU.max, op1=ALU.mult,
             )
-            nc.gpsimd.tensor_tensor(
-                out=g_inv[:, tiles], in0=g_square[:, tiles], in1=INVERSE_ROOT[:, tiles], op=ALU.pow
-            )
+            nc.scalar.activation(out=rough[:], in_=safe[:], func=ACT.Sqrt, scale=-2.0)
+            return safe, rough, guess, ratio, inverse
 
-        def row_norms(h):
-            tiles = slice(4 * h, 4 * (h + 1))
+        def newton(safe, rough, guess, ratio, inverse):
+            nc.vector.reciprocal(out=guess[:], in_=rough[:])
+            nc.gpsimd.tensor_tensor(out=ratio[:], in0=guess[:], in1=guess[:], op=ALU.mult)
+            nc.gpsimd.tensor_tensor(out=ratio[:], in0=ratio[:], in1=safe[:], op=ALU.mult)
             nc.gpsimd.tensor_scalar(
-                out=x_square[:, tiles], in0=x_half[:, tiles], scalar1=TINY_SQ, scalar2=2.0,
-                op0=ALU.max, op1=ALU.mult,
+                out=ratio[:], in0=ratio[:], scalar1=1.0, scalar2=1.5, op0=ALU.mult, op1=ALU.add
             )
-            nc.gpsimd.tensor_tensor(
-                out=x_inv[:, tiles], in0=x_square[:, tiles], in1=INVERSE_ROOT[:, tiles], op=ALU.pow
-            )
+            nc.gpsimd.tensor_tensor(out=inverse[:], in0=guess[:], in1=ratio[:], op=ALU.mult)
+            return inverse
+
+        def class_norms(h):
+            return rough_roots(g_half, slice(4 * h, 4 * (h + 1)), "g%d" % h)
+
+        def row_roots(h):
+            return rough_roots(x_half, slice(4 * h, 4 * (h + 1)), "x%d" % h)
+
+        def row_norms(h, roots):
+            tiles = slice(4 * h, 4 * (h + 1))
+            x_inv = newton(*roots)
             for gamma, scaled in ((GAMMA, gamma_inv), (-GAMMA, minus_gamma_inv)):
                 nc.gpsimd.tensor_scalar(
-                    out=scaled[:, tiles], in0=x_inv[:, tiles], scalar1=gamma, scalar2=1.0,
+                    out=scaled[:, tiles], in0=x_inv[:], scalar1=gamma, scalar2=1.0,
                     op0=ALU.mult, op1=ALU.mult,
                 )
 
         def row_cap(i):
             col = slice(i, i + 1)
-            nc.gpsimd.tensor_tensor(
-                out=x_norm[:, col], in0=x_half[:, col], in1=ROOT[:, col], op=ALU.pow
-            )
-            nc.gpsimd.tensor_scalar(
-                out=x_cap[:, col], in0=x_norm[:, col], scalar1=2.0**0.5 / EPS, scalar2=1.0,
-                op0=ALU.mult, op1=ALU.mult,
+            nc.scalar.activation(
+                out=x_cap[:, col], in_=x_half[:, col], func=ACT.Sqrt,
+                scale=2.0 / (EPS * EPS), bias=cap_floor[:],
             )
 
         def window(i):
             col = slice(i, i + 1)
-            nc.gpsimd.tensor_tensor(
-                out=root_least[:, col], in0=least[:, col], in1=ROOT[:, col], op=ALU.pow
+            nc.scalar.activation(out=nearest[:, col], in_=least[:, col], func=ACT.Sqrt, scale=2.0)
+            nc.scalar.activation(
+                out=unit[:, col], in_=nearest[:, col], func=ACT.Square,
+                scale=(0.5 / CENTRE) ** 0.5, bias=unit_shift[:],
             )
+            nc.vector.reciprocal(out=zoom[:, col], in_=unit[:, col])
             nc.gpsimd.tensor_scalar(
-                out=unit_root[:, col], in0=root_least[:, col],
-                scalar1=CENTRE**-0.5, scalar2=WINDOW * (0.5 / CENTRE) ** 0.5,
-                op0=ALU.mult, op1=ALU.add,
-            )
-            nc.gpsimd.tensor_tensor(
-                out=zoom[:, col], in0=unit_root[:, col], in1=INVERSE_SQUARE[:, col], op=ALU.pow
-            )
-            nc.gpsimd.tensor_scalar(
-                out=nearest[:, col], in0=root_least[:, col], scalar1=2.0**0.5, scalar2=1.0,
-                op0=ALU.mult, op1=ALU.mult,
-            )
-            nc.gpsimd.tensor_scalar(
-                out=minus_step[:, col], in0=unit_root[:, col], scalar1=-(2.0**0.5), scalar2=1.0,
-                op0=ALU.mult, op1=ALU.mult,
+                out=minus_step[:, col], in0=nearest[:, col],
+                scalar1=WINDOW, scalar2=-(CENTRE**-0.5), op0=ALU.add, op1=ALU.mult,
             )
 
         def exponent_shift(i):
@@ -296,19 +294,9 @@ def tile_classifier_kernel(tc, X, grp, out):
 
         def normaliser(i):
             col = slice(i, i + 1)
-            if i + 1 < ROW_TILES:
-                nc.gpsimd.tensor_tensor(
-                    out=sums[:, col], in0=sum_cos[:, col], in1=sum_dist[:, col], op=ALU.mult
-                )
-                nc.gpsimd.tensor_tensor(
-                    out=norm[:, col], in0=sums[:, col], in1=INVERSE[:, col], op=ALU.pow
-                )
-                return norm[:, col]
-            nc.vector.tensor_tensor(
-                out=last_sums[:, col], in0=sum_cos[:, col], in1=sum_dist[:, col], op=ALU.mult
-            )
-            nc.vector.reciprocal(out=last_norm[:, col], in_=last_sums[:, col])
-            return last_norm[:, col]
+            nc.vector.tensor_mul(out=sums[:, col], in0=sum_cos[:, col], in1=sum_dist[:, col])
+            nc.vector.reciprocal(out=norm[:, col], in_=sums[:, col])
+            return norm[:, col]
 
         def square_row(i):
             half_sum_of_squares(x_nat[:, i, :], x_half[:, i : i + 1])
@@ -317,6 +305,8 @@ def tile_classifier_kernel(tc, X, grp, out):
         grouped_pairs = []
         flipped = {}
         class_square = {}
+        g_inv = {}
+        g_roots = []
 
         def class_slot(j):
             return grouped_pairs[j // 2][:, :, K_PASS * (j % 2) : K_PASS * (j % 2 + 1)]
@@ -358,16 +348,19 @@ def tile_classifier_kernel(tc, X, grp, out):
             if j - 3 in CLASSES_ON_TENSOR:
                 half_diagonal(class_square[j - 3][:, :P], g_half[:, j - 3 : j - 2])
             if j in (5, ROW_TILES):
-                class_norms(0 if j == 5 else 1)
+                g_roots.append(class_norms(j // ROW_TILES))
+            if j == 7:
+                g_inv[0] = newton(*g_roots[0])
         for i in range(AHEAD):
             quantise_rows(i, ready[i][:])
-        spread_out(nc.vector.tensor_copy, g_half_all, 0, spread_on_tensor(g_half, 0))
-        half_bank = spread_on_tensor(g_half, 1)
-        inverse_banks = [spread_on_tensor(g_inv, 0)]
+        spread_out(nc.vector.tensor_copy, g_half_all, 0, spread_on_tensor(g_half[:, 0:4]))
+        half_bank = spread_on_tensor(g_half[:, 4:8])
+        inverse_banks = [spread_on_tensor(g_inv[0][:])]
+        g_inv[1] = newton(*g_roots[1])
         spread_out(nc.vector.tensor_copy, g_half_all, 1, half_bank)
         spread_out(nc.scalar.copy, g_inv_all, 0, inverse_banks[0])
         dots = {0: products(0)}
-        inverse_banks.append(spread_on_tensor(g_inv, 1))
+        inverse_banks.append(spread_on_tensor(g_inv[1][:]))
 
         row_square = {}
         for i in range(ROW_TILES):
@@ -380,8 +373,9 @@ def tile_classifier_kernel(tc, X, grp, out):
                 row_square[i + 1] = psum.tile([P, 4, P], F32, name="bank", tag="bank")
                 squares_on_tensor(row_square[i + 1][:, 0, :], ready[i + 1][:])
             half_squared_distances(i, dots[i])
+            if i >= 1:
+                window(i - 1)
             clamp_and_least(i)
-            window(i)
             if i == 0:
                 spread_out(nc.vector.tensor_copy, g_inv_all, 1, inverse_banks[1])
             if i < ROW_TILES - HELD:
@@ -401,16 +395,22 @@ def tile_classifier_kernel(tc, X, grp, out):
                 row_cap(i + 1)
             if later < ROW_TILES:
                 quantise_rows(later, ready[later][:])
+            if i == 2:
+                x_roots = [row_roots(0)]
             if i == 3:
-                row_norms(0)
-        row_norms(1)
-        for i in range(LEAD):
-            largest_cosine(i)
+                row_norms(0, x_roots[0])
+            if i == 5:
+                x_roots.append(row_roots(1))
+            if i == 6:
+                row_norms(1, x_roots[1])
+        largest_cosine(0)
+        window(ROW_TILES - 1)
         root(ROW_TILES - 1)
+        for i in range(1, LEAD):
+            largest_cosine(i)
         for i in range(LEAD):
             exponent_shift(i)
 
-        factors = {}
         for i in range(ROW_TILES):
             exponentials(i)
             if i < HELD:
@@ -418,7 +418,6 @@ def tile_classifier_kernel(tc, X, grp, out):
             if i + LEAD < ROW_TILES:
                 largest_cosine(i + LEAD)
                 exponent_shift(i + LEAD)
-            factors[i] = normaliser(i)
             if i >= 1:
-                weigh_and_store(i - 1, factors[i - 1])
-        weigh_and_store(ROW_TILES - 1, factors[ROW_TILES - 1])
+                weigh_and_store(i - 1, normaliser(i - 1))
+        weigh_and_store(ROW_TILES - 1, normaliser(ROW_TILES - 1))

@@ -19,9 +19,12 @@ PASSES = H // K_PASS
 N_MOVE = 512
 HALVES = C // N_MOVE
 
-CLASSES_ON_TENSOR = (1, 2, 4, 5)
-CLASSES_COPIED_BY_SCALAR = (2, 4, 5)
-ROWS_ON_TENSOR = (2, 4)
+CLASSES_ON_TENSOR = (0, 2)
+CLASSES_COPIED_BY_SCALAR = (2,)
+ROWS_ON_GPSIMD = (5, 7)
+GP_COLUMNS = 512
+GP_START = 9
+T_AHEAD = 2
 SQUARES_AHEAD = 2
 AHEAD = 2
 HELD = 3
@@ -101,9 +104,9 @@ def tile_classifier_kernel(tc, X, grp, out):
                 banks.append(flipped)
             return banks
 
-        def squares_on_tensor(bank, grouped):
+        def squares_on_tensor(bank, grouped, half):
             columns = grouped.rearrange("p g (r t) -> p g r t", t=4)
-            for g in range(PASSES):
+            for g in range(2 * half, 2 * (half + 1)):
                 for t in range(4):
                     nc.tensor.matmul(
                         out=bank, lhsT=columns[:, g, :, t], rhs=columns[:, g, :, t],
@@ -172,6 +175,39 @@ def tile_classifier_kernel(tc, X, grp, out):
                 out=dist[:, i, :], in_=dist[:, i, :], func=ACT.Exp, scale=minus_step[:, col],
                 bias=nearest[:, col], accum_out=sum_dist[:, col],
             )
+
+        halves = small.tile([P, 2], F32, name="halves")
+        nc.vector.memset(halves[:], 0.5)
+
+        def squares_on_gpsimd(i):
+            place = cosine if ROWS_ON_GPSIMD.index(i) % 2 == 0 else dist
+            squares = place[:, ROW_TILES - 2 :, :].rearrange("p a c -> p (a c)")
+            for first in range(0, H, GP_COLUMNS):
+                cols = slice(first, first + GP_COLUMNS)
+                nc.gpsimd.tensor_tensor(
+                    out=squares[:, cols], in0=x_nat[:, i, cols], in1=x_nat[:, i, cols], op=ALU.mult
+                )
+            return squares
+
+        def sum_on_tensor(squares):
+            sums_bank = psum.tile([P, N_MOVE], F32, name="bank", tag="bank")
+            for k in range(H // P):
+                nc.tensor.matmul(
+                    out=sums_bank[:, :P], lhsT=squares[:, P * k : P * (k + 1)], rhs=ident[:],
+                    start=(k == 0), stop=(k == H // P - 1), is_transpose=True,
+                )
+            return sums_bank
+
+        def sum_partials(sums_bank):
+            partial = scrap.tile([P, P], F32, name="partial")
+            nc.scalar.copy(out=partial[:], in_=sums_bank[:, :P])
+            nc.tensor.matmul(
+                out=sums_bank[:, P : P + 2], lhsT=partial[:], rhs=halves[:], start=True, stop=True
+            )
+
+        def fetch_sum(i, sums_bank):
+            nc.scalar.copy(out=x_half[:, i : i + 1], in_=sums_bank[:, P : P + 1])
+            row_cap(i)
 
         def half_diagonal(bank, total):
             masked = scrap.tile([P, P], F32, name="masked")
@@ -307,6 +343,7 @@ def tile_classifier_kernel(tc, X, grp, out):
         class_square = {}
         g_inv = {}
         g_roots = []
+        wide_squares = {}
 
         def class_slot(j):
             return grouped_pairs[j // 2][:, :, K_PASS * (j % 2) : K_PASS * (j % 2 + 1)]
@@ -317,19 +354,27 @@ def tile_classifier_kernel(tc, X, grp, out):
             for bank in range(2):
                 regroup(engine_copy, grouped, bank, banks[bank])
 
-        for j in range(ROW_TILES + AHEAD):
+        def turn(j):
             if j < ROW_TILES:
                 flipped[j] = transposes(g_nat[:, j, :])
-                if j % 2 == 0:
-                    grouped = stage.tile(
-                        [P, PASSES, 2 * K_PASS], BF16, align_bytes=64, name="grouped_pair"
-                    )
-                    grouped_pairs.append(grouped)
-            else:
+            elif j < ROW_TILES + AHEAD:
                 flipped[j] = transposes(x_nat[:, j - ROW_TILES, :])
-            if j - 2 in CLASSES_ON_TENSOR:
-                class_square[j - 2] = psum.tile([P, N_MOVE], F32, name="bank", tag="bank")
-                squares_on_tensor(class_square[j - 2][:, :P], class_slot(j - 2))
+
+        for j in range(T_AHEAD):
+            turn(j)
+        for j in range(ROW_TILES + AHEAD):
+            turn(j + T_AHEAD)
+            if j < ROW_TILES and j % 2 == 0:
+                grouped = stage.tile(
+                    [P, PASSES, 2 * K_PASS], BF16, align_bytes=64, name="grouped_pair"
+                )
+                grouped_pairs.append(grouped)
+            for half in range(2):
+                k = j - 1 - half
+                if k in CLASSES_ON_TENSOR:
+                    if half == 0:
+                        class_square[k] = psum.tile([P, N_MOVE], F32, name="bank", tag="bank")
+                    squares_on_tensor(class_square[k][:, :P], class_slot(k), half)
             if j < ROW_TILES:
                 if j in CLASSES_COPIED_BY_SCALAR:
                     copies(nc.scalar.copy, class_slot(j), flipped[j])
@@ -340,23 +385,25 @@ def tile_classifier_kernel(tc, X, grp, out):
             else:
                 i = j - ROW_TILES
                 ready[i] = stage.tile([P, PASSES, K_PASS], BF16, align_bytes=64, name="grouped", bufs=4)
-                copies(nc.scalar.copy if i == 0 else nc.vector.tensor_copy, ready[i][:], flipped[j])
-                half_sum_of_squares(x_nat[:, i, :], x_half[:, i : i + 1])
-                row_cap(i)
-            if j >= 2 and j % 2 == 0:
-                quantise_class_pair(j // 2 - 1, grouped_pairs[j // 2 - 1][:])
+                copies(nc.vector.tensor_copy, ready[i][:], flipped[j])
+                if i == 0:
+                    square_row(i)
+            if j % 2 == 1 and j < ROW_TILES:
+                quantise_class_pair(j // 2, grouped_pairs[j // 2][:])
+            if j >= ROW_TILES:
+                quantise_rows(i, ready[i][:])
             if j - 3 in CLASSES_ON_TENSOR:
                 half_diagonal(class_square[j - 3][:, :P], g_half[:, j - 3 : j - 2])
-            if j in (5, ROW_TILES):
-                g_roots.append(class_norms(j // ROW_TILES))
-            if j == 7:
-                g_inv[0] = newton(*g_roots[0])
-        for i in range(AHEAD):
-            quantise_rows(i, ready[i][:])
+            if j in (6, ROW_TILES):
+                g_roots.append(class_norms(len(g_roots)))
+            if j in (7, ROW_TILES + 1):
+                g_inv[len(g_inv)] = newton(*g_roots[len(g_inv)])
+            if j == GP_START:
+                for k in ROWS_ON_GPSIMD[:2]:
+                    wide_squares[k] = squares_on_gpsimd(k)
         spread_out(nc.vector.tensor_copy, g_half_all, 0, spread_on_tensor(g_half[:, 0:4]))
         half_bank = spread_on_tensor(g_half[:, 4:8])
         inverse_banks = [spread_on_tensor(g_inv[0][:])]
-        g_inv[1] = newton(*g_roots[1])
         spread_out(nc.vector.tensor_copy, g_half_all, 1, half_bank)
         spread_out(nc.scalar.copy, g_inv_all, 0, inverse_banks[0])
         dots = {0: products(0)}
@@ -365,22 +412,26 @@ def tile_classifier_kernel(tc, X, grp, out):
         row_square = {}
         for i in range(ROW_TILES):
             later = i + AHEAD
+            if later in ROWS_ON_GPSIMD:
+                sum_partials(row_square[later])
             if later < ROW_TILES:
                 flipped[later] = transposes(x_nat[:, later, :])
             if i + 1 < ROW_TILES:
                 dots[i + 1] = products(i + 1)
-            if i + 1 in ROWS_ON_TENSOR:
-                row_square[i + 1] = psum.tile([P, 4, P], F32, name="bank", tag="bank")
-                squares_on_tensor(row_square[i + 1][:, 0, :], ready[i + 1][:])
+            if later + 1 in ROWS_ON_GPSIMD:
+                row_square[later + 1] = sum_on_tensor(wide_squares[later + 1])
+                if later + 4 in ROWS_ON_GPSIMD:
+                    wide_squares[later + 4] = squares_on_gpsimd(later + 4)
             half_squared_distances(i, dots[i])
             if i >= 1:
                 window(i - 1)
             clamp_and_least(i)
             if i == 0:
                 spread_out(nc.vector.tensor_copy, g_inv_all, 1, inverse_banks[1])
+                square_row(1)
             if i < ROW_TILES - HELD:
                 cosines(i, dots[i])
-            if AHEAD <= i + SQUARES_AHEAD < ROW_TILES and i + SQUARES_AHEAD not in ROWS_ON_TENSOR:
+            if AHEAD <= i + SQUARES_AHEAD < ROW_TILES and i + SQUARES_AHEAD not in ROWS_ON_GPSIMD:
                 square_row(i + SQUARES_AHEAD)
             if i == 0:
                 for k in range(AHEAD, SQUARES_AHEAD):
@@ -388,11 +439,10 @@ def tile_classifier_kernel(tc, X, grp, out):
             if later < ROW_TILES:
                 ready[later] = stage.tile([P, PASSES, K_PASS], BF16, align_bytes=64, name="grouped", bufs=4)
                 copies(nc.scalar.copy, ready[later][:], flipped[later])
+            if later in ROWS_ON_GPSIMD:
+                fetch_sum(later, row_square[later])
             if i >= 1:
                 root(i - 1)
-            if i + 1 in ROWS_ON_TENSOR:
-                half_diagonal(row_square[i + 1][:, 0, :], x_half[:, i + 1 : i + 2])
-                row_cap(i + 1)
             if later < ROW_TILES:
                 quantise_rows(later, ready[later][:])
             if i == 2:

@@ -27,6 +27,7 @@ GP_START = 9
 T_AHEAD = 2
 SQUARES_AHEAD = 2
 AHEAD = 2
+TAIL_PIECES = 2
 HELD = 3
 LEAD = 3
 
@@ -92,6 +93,7 @@ def tile_classifier_kernel(tc, X, grp, out):
         )
         top, minus_top = stat("top"), stat("minus_top")
         sum_cos, sum_dist, sums, norm = stat("sum_cos"), stat("sum_dist"), stat("sums"), stat("norm")
+        last_sums = stat("last_sums")
 
         def transposes(natural):
             words = natural.bitcast(F32)
@@ -207,7 +209,6 @@ def tile_classifier_kernel(tc, X, grp, out):
 
         def fetch_sum(i, sums_bank):
             nc.scalar.copy(out=x_half[:, i : i + 1], in_=sums_bank[:, P : P + 1])
-            row_cap(i)
 
         def half_diagonal(bank, total):
             masked = scrap.tile([P, P], F32, name="masked")
@@ -257,12 +258,15 @@ def tile_classifier_kernel(tc, X, grp, out):
                 out=top[:, i : i + 1], in_=cosine[:, i, :], axis=mybir.AxisListType.X, op=ALU.max
             )
 
-        def weigh_and_store(i, factor):
-            nc.vector.scalar_tensor_tensor(
-                out=cosine[:, i, :], in0=cosine[:, i, :], scalar=factor,
-                in1=dist[:, i, :], op0=ALU.mult, op1=ALU.mult,
-            )
-            nc.sync.dma_start(out=out[P * i : P * (i + 1), :], in_=cosine[:, i, :])
+        def weigh_and_store(i):
+            width = C // TAIL_PIECES if i + 1 == ROW_TILES else C
+            for first in range(0, C, width):
+                cols = slice(first, first + width)
+                nc.vector.scalar_tensor_tensor(
+                    out=cosine[:, i, cols], in0=cosine[:, i, cols], scalar=norm[:, i : i + 1],
+                    in1=dist[:, i, cols], op0=ALU.mult, op1=ALU.mult,
+                )
+                nc.sync.dma_start(out=out[P * i : P * (i + 1), cols], in_=cosine[:, i, cols])
 
         def rough_roots(half_squares, tiles, name):
             width = tiles.stop - tiles.start
@@ -312,6 +316,8 @@ def tile_classifier_kernel(tc, X, grp, out):
         def window(i):
             col = slice(i, i + 1)
             nc.scalar.activation(out=nearest[:, col], in_=least[:, col], func=ACT.Sqrt, scale=2.0)
+            if i + 2 < ROW_TILES:
+                row_cap(i + 2)
             nc.scalar.activation(
                 out=unit[:, col], in_=nearest[:, col], func=ACT.Square,
                 scale=(0.5 / CENTRE) ** 0.5, bias=unit_shift[:],
@@ -328,15 +334,19 @@ def tile_classifier_kernel(tc, X, grp, out):
                 out=minus_top[:, col], in0=top[:, col], in1=minus_gamma_inv[:, col], op=ALU.mult
             )
 
-        def normaliser(i):
+        def sum_product(i):
+            engine, place = (nc.gpsimd, sums) if i + 1 < ROW_TILES else (nc.vector, last_sums)
             col = slice(i, i + 1)
-            nc.vector.tensor_mul(out=sums[:, col], in0=sum_cos[:, col], in1=sum_dist[:, col])
-            nc.vector.reciprocal(out=norm[:, col], in_=sums[:, col])
-            return norm[:, col]
+            engine.tensor_tensor(
+                out=place[:, col], in0=sum_cos[:, col], in1=sum_dist[:, col], op=ALU.mult
+            )
+            return place[:, col]
+
+        def normaliser(i, total):
+            nc.vector.reciprocal(out=norm[:, i : i + 1], in_=total)
 
         def square_row(i):
             half_sum_of_squares(x_nat[:, i, :], x_half[:, i : i + 1])
-            row_cap(i)
 
         grouped_pairs = []
         flipped = {}
@@ -428,6 +438,7 @@ def tile_classifier_kernel(tc, X, grp, out):
             clamp_and_least(i)
             if i == 0:
                 spread_out(nc.vector.tensor_copy, g_inv_all, 1, inverse_banks[1])
+                row_cap(0)
                 square_row(1)
             if i < ROW_TILES - HELD:
                 cosines(i, dots[i])
@@ -439,6 +450,8 @@ def tile_classifier_kernel(tc, X, grp, out):
             if later < ROW_TILES:
                 ready[later] = stage.tile([P, PASSES, K_PASS], BF16, align_bytes=64, name="grouped", bufs=4)
                 copies(nc.scalar.copy, ready[later][:], flipped[later])
+            if i == 0:
+                row_cap(1)
             if later in ROWS_ON_GPSIMD:
                 fetch_sum(later, row_square[later])
             if i >= 1:
@@ -463,11 +476,16 @@ def tile_classifier_kernel(tc, X, grp, out):
 
         for i in range(ROW_TILES):
             exponentials(i)
-            if i < HELD:
-                cosines(ROW_TILES - HELD + i, dots[ROW_TILES - HELD + i])
+            if i >= 1:
+                total = sum_product(i - 1)
             if i + LEAD < ROW_TILES:
                 largest_cosine(i + LEAD)
                 exponent_shift(i + LEAD)
             if i >= 1:
-                weigh_and_store(i - 1, normaliser(i - 1))
-        weigh_and_store(ROW_TILES - 1, normaliser(ROW_TILES - 1))
+                normaliser(i - 1, total)
+            if i < HELD:
+                cosines(ROW_TILES - HELD + i, dots[ROW_TILES - HELD + i])
+            if i >= 1:
+                weigh_and_store(i - 1)
+        normaliser(ROW_TILES - 1, sum_product(ROW_TILES - 1))
+        weigh_and_store(ROW_TILES - 1)

@@ -19,10 +19,10 @@ PASSES = H // K_PASS
 N_MOVE = 512
 HALVES = C // N_MOVE
 
-CLASSES_ON_TENSOR = (0, 2)
-CLASSES_COPIED_BY_SCALAR = (2,)
+CLASSES_ON_TENSOR = (1, 4)
+CLASSES_COPIED_BY_SCALAR = (4,)
 ROWS_ON_GPSIMD = (5, 7)
-GP_COLUMNS = 512
+GP_COLUMNS = 256
 GP_START = 9
 T_AHEAD = 2
 SQUARES_AHEAD = 2
@@ -402,8 +402,8 @@ def tile_classifier_kernel(tc, X, grp, out):
                 quantise_class_pair(j // 2, grouped_pairs[j // 2][:])
             if j >= ROW_TILES:
                 quantise_rows(i, ready[i][:])
-            if j - 3 in CLASSES_ON_TENSOR:
-                half_diagonal(class_square[j - 3][:, :P], g_half[:, j - 3 : j - 2])
+            if j - 4 in CLASSES_ON_TENSOR:
+                half_diagonal(class_square[j - 4][:, :P], g_half[:, j - 4 : j - 3])
             if j in (6, ROW_TILES):
                 g_roots.append(class_norms(len(g_roots)))
             if j in (7, ROW_TILES + 1):
@@ -422,10 +422,10 @@ def tile_classifier_kernel(tc, X, grp, out):
         row_square = {}
         for i in range(ROW_TILES):
             later = i + AHEAD
-            if later in ROWS_ON_GPSIMD:
-                sum_partials(row_square[later])
             if later < ROW_TILES:
                 flipped[later] = transposes(x_nat[:, later, :])
+            if later in ROWS_ON_GPSIMD:
+                sum_partials(row_square[later])
             if i + 1 < ROW_TILES:
                 dots[i + 1] = products(i + 1)
             if later + 1 in ROWS_ON_GPSIMD:
@@ -435,13 +435,13 @@ def tile_classifier_kernel(tc, X, grp, out):
             half_squared_distances(i, dots[i])
             if i >= 1:
                 window(i - 1)
-            clamp_and_least(i)
             if i == 0:
                 spread_out(nc.vector.tensor_copy, g_inv_all, 1, inverse_banks[1])
                 row_cap(0)
                 square_row(1)
             if i < ROW_TILES - HELD:
                 cosines(i, dots[i])
+            clamp_and_least(i)
             if AHEAD <= i + SQUARES_AHEAD < ROW_TILES and i + SQUARES_AHEAD not in ROWS_ON_GPSIMD:
                 square_row(i + SQUARES_AHEAD)
             if i == 0:

@@ -22,7 +22,7 @@ HALVES = C // N_MOVE
 CLASSES_ON_TENSOR = (1, 4)
 CLASSES_COPIED_BY_SCALAR = (4,)
 ROWS_ON_GPSIMD = (5, 7)
-GP_COLUMNS = 256
+GP_COLUMNS = 512
 GP_START = 9
 T_AHEAD = 2
 SQUARES_AHEAD = 2

from contextlib import ExitStack

import concourse.mybir as mybir
from concourse.masks import make_identity

F32 = mybir.dt.float32
BF16 = mybir.dt.bfloat16
U32 = mybir.dt.uint32
U8 = mybir.dt.uint8
FP8X4 = mybir.dt.float8_e4m3fn_x4
ACT = mybir.ActivationFunctionType
ALU = mybir.AluOpType

P = 128
B, H, C = 1024, 2048, 1024
ROW_TILES = B // P
K_PASS = 4 * P
PASSES = H // K_PASS
N_MOVE = 512
HALVES = C // N_MOVE

CLASSES_ON_TENSOR = (1, 4)
CLASSES_COPIED_BY_SCALAR = (4,)
ROWS_ON_GPSIMD = (5, 7)
GP_COLUMNS = 512
GP_START = 9
T_AHEAD = 2
SQUARES_AHEAD = 2
AHEAD = 2
TAIL_PIECES = 2
HELD = 3
LEAD = 3

GAMMA = 100.0
EPS = 1e-8
TINY_SQ = 1e-30
TINY_D2 = 1e-30
CENTRE = 1.875
WINDOW = 4.0

ROOT_HALF = 0.5**0.5

FLOPS = 2 * B * C * H


def tile_classifier_kernel(tc, X, grp, out):
    nc = tc.nc
    with ExitStack() as ctx:
        keep = ctx.enter_context(tc.tile_pool(name="keep", bufs=1))
        small = ctx.enter_context(tc.tile_pool(name="small", bufs=1))
        stage = ctx.enter_context(tc.tile_pool(name="stage", bufs=3))
        scrap = ctx.enter_context(tc.tile_pool(name="scrap", bufs=2))
        psum = ctx.enter_context(tc.psum_pool(name="psum", bufs=8))
        ctx.enter_context(tc.manual_schedule())

        g_nat = keep.tile([P, ROW_TILES, H], BF16, name="g_nat")
        x_nat = keep.tile([P, ROW_TILES, H], BF16, name="x_nat")
        for j in range(ROW_TILES):
            nc.sync.dma_start(out=g_nat[:, j, :], in_=grp[P * j : P * (j + 1), :])
        for i in range(ROW_TILES):
            nc.sync.dma_start(out=x_nat[:, i, :], in_=X[P * i : P * (i + 1), :])

        ident = keep.tile([P, P], F32, name="ident")
        make_identity(nc, ident[:])

        warm = small.tile([P, 1], F32, name="warm")
        nc.vector.memset(warm[:], 1.0)
        nc.scalar.activation(out=warm[:], in_=warm[:], func=ACT.Sqrt)
        cap_floor = small.tile([P, 1], F32, name="cap_floor")
        nc.vector.memset(cap_floor[:], TINY_SQ / (EPS * EPS))
        unit_shift = small.tile([P, 1], F32, name="unit_shift")
        nc.vector.memset(unit_shift[:], 1.0)
        nc.vector.tensor_scalar_mul(
            out=unit_shift[:], in0=unit_shift[:], scalar1=WINDOW * (0.5 / CENTRE) ** 0.5
        )

        g_codes = keep.tile([P, PASSES, C], U32, align_bytes=64, name="g_codes")
        g_scales = keep.tile([P, PASSES, C], U8, align_bytes=64, name="g_scales")
        x_codes = keep.tile([P, ROW_TILES, PASSES * P], U32, align_bytes=64, name="x_codes")
        x_scales = keep.tile([P, ROW_TILES, PASSES * P], U8, align_bytes=64, name="x_scales")
        cosine = keep.tile([P, ROW_TILES, C], F32, name="cosine")
        dist = keep.tile([P, ROW_TILES, C], F32, name="dist")
        g_half_all = keep.tile([P, C], F32, name="g_half_all")
        g_inv_all = keep.tile([P, C], F32, name="g_inv_all")

        def stat(name):
            return small.tile([P, ROW_TILES], F32, name=name)

        g_half, x_half, x_cap = stat("g_half"), stat("x_half"), stat("x_cap")
        gamma_inv, minus_gamma_inv = stat("gamma_inv"), stat("minus_gamma_inv")
        least, nearest, minus_step, unit, zoom = (
            stat("least"), stat("nearest"), stat("minus_step"), stat("unit"), stat("zoom"),
        )
        top, minus_top = stat("top"), stat("minus_top")
        sum_cos, sum_dist, sums, norm = stat("sum_cos"), stat("sum_dist"), stat("sums"), stat("norm")
        last_sums = stat("last_sums")

        def transposes(natural):
            words = natural.bitcast(F32)
            banks = []
            for bank in range(2):
                flipped = psum.tile([P, 4, P], F32, name="bank", tag="bank")
                for w in range(4):
                    first = (4 * bank + w) * P
                    nc.tensor.transpose(flipped[:, w, :], words[:, first : first + P], ident[:])
                banks.append(flipped)
            return banks

        def squares_on_tensor(bank, grouped, half):
            columns = grouped.rearrange("p g (r t) -> p g r t", t=4)
            for g in range(2 * half, 2 * (half + 1)):
                for t in range(4):
                    nc.tensor.matmul(
                        out=bank, lhsT=columns[:, g, :, t], rhs=columns[:, g, :, t],
                        start=(g == 0 and t == 0), stop=(g == PASSES - 1 and t == 3),
                    )

        def products(i):
            dots = []
            for h in range(HALVES):
                cols = slice(N_MOVE * h, N_MOVE * (h + 1))
                dot = psum.tile([P, N_MOVE], F32, name="bank", tag="bank")
                for g in range(PASSES):
                    rows = slice(P * g, P * (g + 1))
                    nc.tensor.matmul_mx(
                        out=dot[:],
                        lhsT=x_codes[:, i, rows].bitcast(FP8X4),
                        lhsT_scale=x_scales[:, i, rows],
                        rhs=g_codes[:, g, cols].bitcast(FP8X4),
                        rhs_scale=g_scales[:, g, cols],
                        start=(g == 0),
                        stop=(g == PASSES - 1),
                    )
                dots.append(dot)
            return dots

        def spread_on_tensor(per_class):
            flipped = psum.tile([P, 4, P], F32, name="bank", tag="bank")
            for w in range(4):
                nc.tensor.transpose(
                    flipped[:, w, :], per_class[:, w : w + 1].to_broadcast([P, P]), ident[:]
                )
            return flipped

        def regroup(copy, grouped, bank, flipped):
            copy(
                out=grouped.bitcast(F32)[:, 2 * bank : 2 * bank + 2, :].rearrange(
                    "p g (r u) -> p g r u", u=2
                ),
                in_=flipped[:].rearrange("p (g u) r -> p g r u", u=2),
            )

        def spread_out(copy, spread, h, flipped):
            copy(
                out=spread[:, N_MOVE * h : N_MOVE * (h + 1)],
                in_=flipped[:].rearrange("p w c -> p (w c)"),
            )

        def half_sum_of_squares(natural, total):
            squares = scrap.tile([P, H], BF16, name="squares")
            nc.scalar.activation(
                out=squares[:], in_=natural, func=ACT.Square, scale=ROOT_HALF, accum_out=total
            )

        def root(i):
            nc.scalar.activation(
                out=dist[:, i, :], in_=dist[:, i, :], func=ACT.Sqrt, scale=zoom[:, i : i + 1]
            )

        def exponentials(i):
            col = slice(i, i + 1)
            nc.scalar.activation(
                out=cosine[:, i, :], in_=cosine[:, i, :], func=ACT.Exp, scale=gamma_inv[:, col],
                bias=minus_top[:, col], accum_out=sum_cos[:, col],
            )
            nc.scalar.activation(
                out=dist[:, i, :], in_=dist[:, i, :], func=ACT.Exp, scale=minus_step[:, col],
                bias=nearest[:, col], accum_out=sum_dist[:, col],
            )

        halves = small.tile([P, 2], F32, name="halves")
        nc.vector.memset(halves[:], 0.5)

        def squares_on_gpsimd(i):
            place = cosine if ROWS_ON_GPSIMD.index(i) % 2 == 0 else dist
            squares = place[:, ROW_TILES - 2 :, :].rearrange("p a c -> p (a c)")
            for first in range(0, H, GP_COLUMNS):
                cols = slice(first, first + GP_COLUMNS)
                nc.gpsimd.tensor_tensor(
                    out=squares[:, cols], in0=x_nat[:, i, cols], in1=x_nat[:, i, cols], op=ALU.mult
                )
            return squares

        def sum_on_tensor(squares):
            sums_bank = psum.tile([P, N_MOVE], F32, name="bank", tag="bank")
            for k in range(H // P):
                nc.tensor.matmul(
                    out=sums_bank[:, :P], lhsT=squares[:, P * k : P * (k + 1)], rhs=ident[:],
                    start=(k == 0), stop=(k == H // P - 1), is_transpose=True,
                )
            return sums_bank

        def sum_partials(sums_bank):
            partial = scrap.tile([P, P], F32, name="partial")
            nc.scalar.copy(out=partial[:], in_=sums_bank[:, :P])
            nc.tensor.matmul(
                out=sums_bank[:, P : P + 2], lhsT=partial[:], rhs=halves[:], start=True, stop=True
            )

        def fetch_sum(i, sums_bank):
            nc.scalar.copy(out=x_half[:, i : i + 1], in_=sums_bank[:, P : P + 1])

        def half_diagonal(bank, total):
            masked = scrap.tile([P, P], F32, name="masked")
            nc.vector.scalar_tensor_tensor(
                out=masked[:], in0=bank, scalar=0.5, in1=ident[:],
                op0=ALU.mult, op1=ALU.mult, accum_out=total,
            )

        def quantise_class_pair(pair, grouped):
            cols = slice(2 * P * pair, 2 * P * (pair + 1))
            for g in range(PASSES):
                nc.vector.quantize_mx(
                    out=g_codes[:, g, cols].bitcast(FP8X4), scales=g_scales[:, g, cols],
                    in_=grouped[:, g, :],
                )

        def quantise_rows(i, grouped):
            nc.vector.quantize_mx(
                out=x_codes[:, i, :].bitcast(FP8X4), scales=x_scales[:, i, :],
                in_=grouped.rearrange("p g r -> p (g r)"),
            )

        def half_squared_distances(i, dots):
            for h in range(HALVES):
                cols = slice(N_MOVE * h, N_MOVE * (h + 1))
                nc.vector.scalar_tensor_tensor(
                    out=dist[:, i, cols], in0=g_half_all[:, cols], scalar=x_half[:, i : i + 1],
                    in1=dots[h][:], op0=ALU.add, op1=ALU.subtract,
                )

        def clamp_and_least(i):
            nc.vector.tensor_scalar(
                out=dist[:, i, :], in0=dist[:, i, :], scalar1=TINY_D2, scalar2=None,
                op0=ALU.max, op1=ALU.min, accum_out=least[:, i : i + 1],
            )

        def cosines(i, dots):
            for h in range(HALVES):
                cols = slice(N_MOVE * h, N_MOVE * (h + 1))
                nc.vector.scalar_tensor_tensor(
                    out=cosine[:, i, cols], in0=g_inv_all[:, cols], scalar=x_cap[:, i : i + 1],
                    in1=dots[h][:], op0=ALU.min, op1=ALU.mult,
                )

        def largest_cosine(i):
            nc.vector.tensor_reduce(
                out=top[:, i : i + 1], in_=cosine[:, i, :], axis=mybir.AxisListType.X, op=ALU.max
            )

        def weigh_and_store(i):
            width = C // TAIL_PIECES if i + 1 == ROW_TILES else C
            for first in range(0, C, width):
                cols = slice(first, first + width)
                nc.vector.scalar_tensor_tensor(
                    out=cosine[:, i, cols], in0=cosine[:, i, cols], scalar=norm[:, i : i + 1],
                    in1=dist[:, i, cols], op0=ALU.mult, op1=ALU.mult,
                )
                nc.sync.dma_start(out=out[P * i : P * (i + 1), cols], in_=cosine[:, i, cols])

        def rough_roots(half_squares, tiles, name):
            width = tiles.stop - tiles.start
            safe, rough, guess, ratio, inverse = (
                small.tile([P, width], F32, name=name + part)
                for part in ("_safe", "_rough", "_guess", "_ratio", "_inverse")
            )
            nc.gpsimd.tensor_scalar(
                out=safe[:], in0=half_squares[:, tiles], scalar1=TINY_SQ, scalar2=-1.0,
                op0=ALU.max, op1=ALU.mult,
            )
            nc.scalar.activation(out=rough[:], in_=safe[:], func=ACT.Sqrt, scale=-2.0)
            return safe, rough, guess, ratio, inverse

        def newton(safe, rough, guess, ratio, inverse):
            nc.vector.reciprocal(out=guess[:], in_=rough[:])
            nc.gpsimd.tensor_tensor(out=ratio[:], in0=guess[:], in1=guess[:], op=ALU.mult)
            nc.gpsimd.tensor_tensor(out=ratio[:], in0=ratio[:], in1=safe[:], op=ALU.mult)
            nc.gpsimd.tensor_scalar(
                out=ratio[:], in0=ratio[:], scalar1=1.0, scalar2=1.5, op0=ALU.mult, op1=ALU.add
            )
            nc.gpsimd.tensor_tensor(out=inverse[:], in0=guess[:], in1=ratio[:], op=ALU.mult)
            return inverse

        def class_norms(h):
            return rough_roots(g_half, slice(4 * h, 4 * (h + 1)), "g%d" % h)

        def row_roots(h):
            return rough_roots(x_half, slice(4 * h, 4 * (h + 1)), "x%d" % h)

        def row_norms(h, roots):
            tiles = slice(4 * h, 4 * (h + 1))
            x_inv = newton(*roots)
            for gamma, scaled in ((GAMMA, gamma_inv), (-GAMMA, minus_gamma_inv)):
                nc.gpsimd.tensor_scalar(
                    out=scaled[:, tiles], in0=x_inv[:], scalar1=gamma, scalar2=1.0,
                    op0=ALU.mult, op1=ALU.mult,
                )

        def row_cap(i):
            col = slice(i, i + 1)
            nc.scalar.activation(
                out=x_cap[:, col], in_=x_half[:, col], func=ACT.Sqrt,
                scale=2.0 / (EPS * EPS), bias=cap_floor[:],
            )

        def window(i):
            col = slice(i, i + 1)
            nc.scalar.activation(out=nearest[:, col], in_=least[:, col], func=ACT.Sqrt, scale=2.0)
            if i + 2 < ROW_TILES:
                row_cap(i + 2)
            nc.scalar.activation(
                out=unit[:, col], in_=nearest[:, col], func=ACT.Square,
                scale=(0.5 / CENTRE) ** 0.5, bias=unit_shift[:],
            )
            nc.vector.reciprocal(out=zoom[:, col], in_=unit[:, col])
            nc.gpsimd.tensor_scalar(
                out=minus_step[:, col], in0=nearest[:, col],
                scalar1=WINDOW, scalar2=-(CENTRE**-0.5), op0=ALU.add, op1=ALU.mult,
            )

        def exponent_shift(i):
            col = slice(i, i + 1)
            nc.gpsimd.tensor_tensor(
                out=minus_top[:, col], in0=top[:, col], in1=minus_gamma_inv[:, col], op=ALU.mult
            )

        def sum_product(i):
            engine, place = (nc.gpsimd, sums) if i + 1 < ROW_TILES else (nc.vector, last_sums)
            col = slice(i, i + 1)
            engine.tensor_tensor(
                out=place[:, col], in0=sum_cos[:, col], in1=sum_dist[:, col], op=ALU.mult
            )
            return place[:, col]

        def normaliser(i, total):
            nc.vector.reciprocal(out=norm[:, i : i + 1], in_=total)

        def square_row(i):
            half_sum_of_squares(x_nat[:, i, :], x_half[:, i : i + 1])

        grouped_pairs = []
        flipped = {}
        class_square = {}
        g_inv = {}
        g_roots = []
        wide_squares = {}

        def class_slot(j):
            return grouped_pairs[j // 2][:, :, K_PASS * (j % 2) : K_PASS * (j % 2 + 1)]

        ready = {}

        def copies(engine_copy, grouped, banks):
            for bank in range(2):
                regroup(engine_copy, grouped, bank, banks[bank])

        def turn(j):
            if j < ROW_TILES:
                flipped[j] = transposes(g_nat[:, j, :])
            elif j < ROW_TILES + AHEAD:
                flipped[j] = transposes(x_nat[:, j - ROW_TILES, :])

        for j in range(T_AHEAD):
            turn(j)
        for j in range(ROW_TILES + AHEAD):
            turn(j + T_AHEAD)
            if j < ROW_TILES and j % 2 == 0:
                grouped = stage.tile(
                    [P, PASSES, 2 * K_PASS], BF16, align_bytes=64, name="grouped_pair"
                )
                grouped_pairs.append(grouped)
            for half in range(2):
                k = j - 1 - half
                if k in CLASSES_ON_TENSOR:
                    if half == 0:
                        class_square[k] = psum.tile([P, N_MOVE], F32, name="bank", tag="bank")
                    squares_on_tensor(class_square[k][:, :P], class_slot(k), half)
            if j < ROW_TILES:
                if j in CLASSES_COPIED_BY_SCALAR:
                    copies(nc.scalar.copy, class_slot(j), flipped[j])
                else:
                    copies(nc.vector.tensor_copy, class_slot(j), flipped[j])
                if j not in CLASSES_ON_TENSOR:
                    half_sum_of_squares(g_nat[:, j, :], g_half[:, j : j + 1])
            else:
                i = j - ROW_TILES
                ready[i] = stage.tile([P, PASSES, K_PASS], BF16, align_bytes=64, name="grouped", bufs=4)
                copies(nc.vector.tensor_copy, ready[i][:], flipped[j])
                if i == 0:
                    square_row(i)
            if j % 2 == 1 and j < ROW_TILES:
                quantise_class_pair(j // 2, grouped_pairs[j // 2][:])
            if j >= ROW_TILES:
                quantise_rows(i, ready[i][:])
            if j - 4 in CLASSES_ON_TENSOR:
                half_diagonal(class_square[j - 4][:, :P], g_half[:, j - 4 : j - 3])
            if j in (6, ROW_TILES):
                g_roots.append(class_norms(len(g_roots)))
            if j in (7, ROW_TILES + 1):
                g_inv[len(g_inv)] = newton(*g_roots[len(g_inv)])
            if j == GP_START:
                for k in ROWS_ON_GPSIMD[:2]:
                    wide_squares[k] = squares_on_gpsimd(k)
        spread_out(nc.vector.tensor_copy, g_half_all, 0, spread_on_tensor(g_half[:, 0:4]))
        half_bank = spread_on_tensor(g_half[:, 4:8])
        inverse_banks = [spread_on_tensor(g_inv[0][:])]
        spread_out(nc.vector.tensor_copy, g_half_all, 1, half_bank)
        spread_out(nc.scalar.copy, g_inv_all, 0, inverse_banks[0])
        dots = {0: products(0)}
        inverse_banks.append(spread_on_tensor(g_inv[1][:]))

        row_square = {}
        for i in range(ROW_TILES):
            later = i + AHEAD
            if later < ROW_TILES:
                flipped[later] = transposes(x_nat[:, later, :])
            if later in ROWS_ON_GPSIMD:
                sum_partials(row_square[later])
            if i + 1 < ROW_TILES:
                dots[i + 1] = products(i + 1)
            if later + 1 in ROWS_ON_GPSIMD:
                row_square[later + 1] = sum_on_tensor(wide_squares[later + 1])
                if later + 4 in ROWS_ON_GPSIMD:
                    wide_squares[later + 4] = squares_on_gpsimd(later + 4)
            half_squared_distances(i, dots[i])
            if i >= 1:
                window(i - 1)
            if i == 0:
                spread_out(nc.vector.tensor_copy, g_inv_all, 1, inverse_banks[1])
                row_cap(0)
                square_row(1)
            if i < ROW_TILES - HELD:
                cosines(i, dots[i])
            clamp_and_least(i)
            if AHEAD <= i + SQUARES_AHEAD < ROW_TILES and i + SQUARES_AHEAD not in ROWS_ON_GPSIMD:
                square_row(i + SQUARES_AHEAD)
            if i == 0:
                for k in range(AHEAD, SQUARES_AHEAD):
                    square_row(k)
            if later < ROW_TILES:
                ready[later] = stage.tile([P, PASSES, K_PASS], BF16, align_bytes=64, name="grouped", bufs=4)
                copies(nc.scalar.copy, ready[later][:], flipped[later])
            if i == 0:
                row_cap(1)
            if later in ROWS_ON_GPSIMD:
                fetch_sum(later, row_square[later])
            if i >= 1:
                root(i - 1)
            if later < ROW_TILES:
                quantise_rows(later, ready[later][:])
            if i == 2:
                x_roots = [row_roots(0)]
            if i == 3:
                row_norms(0, x_roots[0])
            if i == 5:
                x_roots.append(row_roots(1))
            if i == 6:
                row_norms(1, x_roots[1])
        largest_cosine(0)
        window(ROW_TILES - 1)
        root(ROW_TILES - 1)
        for i in range(1, LEAD):
            largest_cosine(i)
        for i in range(LEAD):
            exponent_shift(i)

        for i in range(ROW_TILES):
            exponentials(i)
            if i >= 1:
                total = sum_product(i - 1)
            if i + LEAD < ROW_TILES:
                largest_cosine(i + LEAD)
                exponent_shift(i + LEAD)
            if i >= 1:
                normaliser(i - 1, total)
            if i < HELD:
                cosines(ROW_TILES - HELD + i, dots[ROW_TILES - HELD + i])
            if i >= 1:
                weigh_and_store(i - 1)
        normaliser(ROW_TILES - 1, sum_product(ROW_TILES - 1))
        weigh_and_store(ROW_TILES - 1)
